import numpy as np
import ml_dtypes


def mxq(x, axis, fmt="e4m3"):
    dtype, down = {"e4m3": (ml_dtypes.float8_e4m3fn, 7), "e5m2": (ml_dtypes.float8_e5m2, 14)}[fmt]
    v = np.moveaxis(np.asarray(x, np.float32).astype(ml_dtypes.bfloat16).astype(np.float64), axis, -1)
    blocks = v.reshape(v.shape[:-1] + (-1, 32))
    amax = np.abs(blocks).max(-1, keepdims=True)
    byte = np.maximum(np.where(amax > 0, np.frexp(amax)[1] - 1 + 127, 0) - down, 1)
    scale = np.exp2(byte - 127.0)
    codes = (blocks / scale).astype(np.float32).astype(dtype).astype(np.float64)
    return np.moveaxis((codes * scale).reshape(v.shape), -1, axis)


WIDE = False


def mx_kscale(k):
    if not WIDE:
        return np.ones(k)
    levels = np.array([18, -18])
    if k % 512:
        return np.exp2(np.random.permutation(np.resize(levels, k // 32))).repeat(32)
    a = np.empty((k // 512, 16))
    for p in range(k // 512):
        a[p, :8] = np.random.permutation(np.resize(levels, 8))
        for g in range(8):
            far = levels[np.abs(levels - a[p, g]) >= 10]
            a[p, g + 8] = far[np.random.randint(len(far))]
    return np.exp2(a.ravel()).repeat(32)


BF16 = ml_dtypes.bfloat16


def bf(x):
    return np.asarray(x, np.float32).astype(BF16)


def f64(x):
    return np.asarray(x).astype(np.float64)


B, T, I, H = 128, 8, 512, 1024


def sigmoid(v):
    return 1.0 / (1.0 + np.exp(-v))


def setup_inputs():
    s = mx_kscale(B * T).reshape(B, T)
    u = mx_kscale(H)
    x0 = bf(np.random.standard_normal((B, T, I)))
    h0 = bf(np.random.standard_normal((B, H)))
    c0 = bf(np.random.standard_normal((B, H)))
    d = {"x": bf(f64(x0) * s[:, :, None]), "h0": h0, "c0": c0}
    pre = {}
    for n in ("f", "i", "g"):
        w0 = bf(np.random.standard_normal((H, I)) / np.sqrt(I))
        d["W_" + n] = bf(f64(w0) / u[:, None])
        d["b_" + n] = bf(np.random.standard_normal(H) * 0.5)
        d["R_" + n] = bf(np.random.standard_normal((H, H)) / np.sqrt(H))
        d["rb_" + n] = bf(np.random.standard_normal(H) * 0.5)
        rec = f64(h0) @ f64(d["R_" + n]).T + f64(d["rb_" + n])
        pre[n] = f64(x0) @ f64(w0).T + f64(d["b_" + n]) + rec[:, None, :]
    d["f_t"] = np.asarray(sigmoid(pre["f"]), np.float32)
    d["i_t"] = np.asarray(sigmoid(pre["i"]), np.float32)
    d["g_t"] = np.asarray(np.tanh(pre["g"]), np.float32)
    s_cols = s.T.reshape(1, T * B)
    s_last = s[:, T - 1:T]
    d["grad_0"] = bf(4.0 * np.random.standard_normal((H, T * B))
                     * np.exp2(np.random.randint(-6, 1, (1, T * B))) / s_cols * u[:, None])
    d["grad_1"] = bf(4.0 * np.random.standard_normal((B, H))
                     * np.exp2(np.random.randint(-6, 1, (B, 1))) / s_last * u)
    d["grad_2"] = bf(4.0 * np.random.standard_normal((B, H))
                     * np.exp2(np.random.randint(-6, 1, (B, 1))) / s_last * u)
    return d


def reference(x, h0, c0, W_f, b_f, R_f, rb_f, W_i, b_i, R_i, rb_i, W_g, b_g, R_g, rb_g,
              f_t, i_t, g_t, grad_0, grad_1, grad_2):
    f, i, g = f64(f_t), f64(i_t), f64(g_t)
    c0v = f64(c0)[:, None, :]
    h = np.tanh(f * c0v + i * g)
    dh = np.transpose(f64(grad_0).T.reshape(T, B, H), (1, 0, 2)).copy()
    dh[:, T - 1, :] += f64(grad_1)
    dc = dh * (1.0 - h * h)
    dc[:, T - 1, :] += f64(grad_2)
    dz_f = (dc * c0v * f * (1.0 - f)).reshape(B * T, H)
    dz_i = (dc * g * i * (1.0 - i)).reshape(B * T, H)
    dz_g = (dc * i * (1.0 - g * g)).reshape(B * T, H)
    dz = np.concatenate([dz_f, dz_i, dz_g], axis=1)
    W = np.concatenate([f64(W_f), f64(W_i), f64(W_g)], axis=0)
    dx = (mxq(dz, 1, "e5m2") @ mxq(W, 0, "e4m3")).reshape(B, T, I)
    xq = mxq(f64(x).reshape(B * T, I), 0, "e4m3")
    dW = mxq(dz, 0, "e5m2").T @ xq
    return dx, dW[:H], dW[H:2 * H], dW[2 * H:]

@@ -1,0 +1,477 @@
+from contextlib import ExitStack
+
+import concourse.mybir as mybir
+from concourse.masks import make_identity
+
+B, T, I, H = 128, 8, 512, 1024
+TOKENS = B * T
+FLOPS = 2 * 2 * TOKENS * 3 * H * I
+BYTES = 3 * TOKENS * H * 4 + TOKENS * H * 2 + 3 * B * H * 2 + 3 * H * I * 2 + TOKENS * I * 2 + (TOKENS + 3 * H) * I * 4
+
+F32 = mybir.dt.float32
+BF16 = mybir.dt.bfloat16
+U32 = mybir.dt.uint32
+U8 = mybir.dt.uint8
+E4M3 = mybir.dt.float8_e4m3fn_x4
+E5M2 = mybir.dt.float8_e5m2_x4
+ALU = mybir.AluOpType
+ACT = mybir.ActivationFunctionType
+
+P = 128
+PACK = 4
+K_PASS = P * PACK
+CW = 256
+CHUNKS = 8
+SPLIT = 256
+GATE_F, GATE_I, GATE_G = 0, 1, 2
+GATE_ORDER = (GATE_I, GATE_G, GATE_F)
+
+
+def tile_lstm_cell_pa_v_kernel(
+    tc, x, h0, c0, W_f, b_f, R_f, rb_f, W_i, b_i, R_i, rb_i, W_g, b_g, R_g, rb_g,
+    f_t, i_t, g_t, grad_0, grad_1, grad_2, out_0, out_1, out_2, out_3,
+):
+    nc = tc.nc
+    weights = (W_f, W_i, W_g)
+    dw_out = (out_1, out_2, out_3)
+
+    def by_pass(ap):
+        return ap.rearrange("b t w -> (b t) w").rearrange("(g p j) w -> g p j w", g=2, j=PACK)
+
+    saved = {"f": by_pass(f_t), "i": by_pass(i_t), "g": by_pass(g_t)}
+    x_rows = by_pass(x)
+    dx_rows = by_pass(out_0)
+    grad_cols = grad_0.rearrange("f (t g b) -> f t g b", t=T, g=2)
+
+    with ExitStack() as ctx:
+        sb = ctx.enter_context(tc.tile_pool(name="sb", bufs=1))
+        ps = ctx.enter_context(tc.psum_pool(name="ps", bufs=1))
+        ctx.enter_context(tc.manual_schedule())
+
+        counters = {}
+
+        def ring(kind, slots, shape, dtype):
+            k = counters.get(kind, 0)
+            counters[kind] = k + 1
+            tag = "%s%d" % (kind, k % slots)
+            return sb.tile(shape, dtype, name=tag, tag=tag, align_bytes=64)
+
+        def bank(kind, shape, dtype):
+            k = counters.get(kind, 0)
+            counters[kind] = k + 1
+            tag = "%s%d" % (kind, k % 2)
+            return ps.tile(shape, dtype, name=tag, tag=tag)
+
+        def half(n):
+            return n // 4
+
+        def tpass(n):
+            return (n // 2) % 2
+
+        def col0(n):
+            return (2 * half(n) + n % 2) * CW
+
+        tiles = {}
+
+        def load_saved(kind, slots, n):
+            if n >= CHUNKS:
+                return
+            t = ring("in_" + kind, slots, [P, PACK, CW], F32)
+            nc.sync.dma_start(out=t[:], in_=saved[kind][tpass(n), :, :, col0(n):col0(n) + CW])
+            tiles[kind, n] = t
+
+        def load_f(n):
+            load_saved("f", 4, n)
+
+        def load_ig(n):
+            load_saved("i", 3, n)
+            load_saved("g", 2, n)
+
+        def load_grad(n):
+            if n >= CHUNKS:
+                return
+            t = ring("grad", 3, [P, 2, T, B // 2], BF16)
+            for ft in range(2):
+                r0 = col0(n) + ft * P
+                nc.sync.dma_start(out=t[:, ft, :, :], in_=grad_cols[r0:r0 + P, :, tpass(n), :])
+            tiles["grad", n] = t
+
+        def load_quarter(q):
+            if q >= 4:
+                return
+            h, g = divmod(q, 2)
+            rows, cols = slice(64 * g, 64 * (g + 1)), slice(h * K_PASS, (h + 1) * K_PASS)
+            t = ring("c0_", 2, [P, K_PASS], BF16)
+            for th in range(2):
+                nc.sync.dma_start(out=t[th:P:2, :], in_=c0[rows, cols])
+            tiles["c0", q] = t
+
+        def load_last_step(q):
+            h, g = divmod(q, 2)
+            rows, cols = slice(64 * g, 64 * (g + 1)), slice(h * K_PASS, (h + 1) * K_PASS)
+            for k, src in enumerate((grad_1, grad_2)):
+                nc.sync.dma_start(out=last_rows[1:P:2, k, :], in_=src[rows, cols])
+
+        def load_operand(k):
+            t = ring("raw", 3, [P, PACK, I], BF16)
+            if k < 2:
+                src = x_rows[k]
+            else:
+                h, gate = divmod(k - 2, 3)
+                src = weights[gate][h * K_PASS:(h + 1) * K_PASS, :].rearrange("(p j) w -> p j w", j=PACK)
+            nc.sync.dma_start(out=t[:], in_=src)
+            tiles["raw", k] = t
+
+        def interleave(engine, dst, src):
+            d = dst.rearrange("p (c i) j -> p c j i", i=4)
+            s = src.rearrange("p j (c i) -> p c j i", i=4)
+            if engine == "scalar":
+                nc.scalar.copy(out=d, in_=s)
+            else:
+                nc.vector.tensor_copy(out=d, in_=s)
+
+        def group_operand(k, engine, lo, hi):
+            if ("grouped", k) not in tiles:
+                tiles["grouped", k] = ring("opg", 2, [P, I, PACK], BF16)
+            if hi > lo:
+                interleave(engine, tiles["grouped", k][:, lo:hi, :], tiles["raw", k][:, :, lo:hi])
+
+        op_codes = sb.tile([P, 8, I], U32, name="op_codes", align_bytes=64)
+        op_scales = sb.tile([P, 8, I], U8, name="op_scales", align_bytes=64)
+
+        def quantise_operand(k):
+            nc.vector.quantize_mx(
+                out=op_codes[:, k, :].bitcast(E4M3), scales=op_scales[:, k, :],
+                in_=tiles["grouped", k][:].rearrange("p w j -> p (w j)"),
+            )
+
+        ident = sb.tile([P, P], F32, name="ident", align_bytes=64)
+        ident_bf = sb.tile([P, P], BF16, name="ident_bf", align_bytes=64)
+        last_rows = sb.tile([P, 2, K_PASS], BF16, name="last_rows", align_bytes=64)
+
+        def turn_last_step(q):
+            bk = bank("tr", [P, 2, 4, P], BF16)
+            for k in range(2):
+                for ft in range(4):
+                    nc.tensor.transpose(bk[:, k, ft, :], last_rows[:, k, ft * P:(ft + 1) * P], ident_bf[:])
+            g1_t = ring("g1_t", 2, [P, 4, P], BF16)
+            g2_neg_t = ring("g2_neg_t", 2, [P, 4, P], F32)
+            nc.scalar.copy(out=g1_t[:], in_=bk[:, 0, :, :])
+            nc.scalar.activation(out=g2_neg_t[:], in_=bk[:, 1, :, :], func=ACT.Copy, scale=-1.0)
+            tiles["g1_t", q], tiles["g2_neg_t", q] = g1_t, g2_neg_t
+
+        def prod_a(n, engine):
+            if n >= CHUNKS:
+                return
+            a = ring("a", 2, [P, PACK, CW], F32)
+            c0_b = tiles["c0", n // 2][:, (n % 2) * CW:(n % 2 + 1) * CW].unsqueeze(1).to_broadcast([P, PACK, CW])
+            engine.tensor_tensor(out=a[:], in0=tiles["f", n][:], in1=c0_b, op=ALU.mult)
+            tiles["a", n] = a
+
+        def prod_b(n):
+            b = ring("b", 2, [P, PACK, CW], F32)
+            nc.vector.tensor_tensor(out=b[:], in0=tiles["i", n][:], in1=tiles["g", n][:], op=ALU.mult)
+            tiles["b", n] = b
+
+        def square_g(n):
+            sg = ring("sg", 2, [P, PACK, CW], F32)
+            nc.scalar.activation(out=sg[:], in_=tiles["g", n][:], func=ACT.Square)
+            tiles["sg", n] = sg
+
+        def add_transposed(out, terms):
+            for k, term in enumerate(terms):
+                nc.tensor.matmul(out, lhsT=term, rhs=ident[:], is_transpose=True,
+                                 start=(k == 0), stop=(k == len(terms) - 1))
+
+        def cell_state(n):
+            banks = []
+            for ft in range(2):
+                bk = bank("ct", [P, PACK, P], F32)
+                for j in range(PACK):
+                    cols = slice(ft * P, (ft + 1) * P)
+                    add_transposed(bk[:, j, :], [tiles["a", n][:, j, cols], tiles["b", n][:, j, cols]])
+                banks.append(bk)
+            tiles["ct", n] = banks
+
+        def tanh_c(n):
+            hs = ring("hs", 1, [P, 2, PACK, P], F32)
+            for ft in range(2):
+                nc.scalar.activation(out=hs[:, ft, :, :], in_=tiles["ct", n][ft][:], func=ACT.Tanh)
+            tiles["hs", n] = hs
+
+        def square_h(n):
+            hs = tiles["hs", n]
+            nc.scalar.activation(out=hs[:], in_=hs[:], func=ACT.Square)
+
+        def minus_one_times(out, in0, in1):
+            nc.vector.scalar_tensor_tensor(out=out, in0=in0, scalar=1.0, in1=in1, op0=ALU.subtract, op1=ALU.mult)
+
+        def dc_turned(n):
+            hs, gr = tiles["hs", n], tiles["grad", n]
+            dct = ring("dct", 1, [P, 2, PACK, P], F32)
+            extra = ring("extra", 1, [P, 2, P], F32)
+            for ft in range(2):
+                minus_one_times(
+                    dct[:, ft, :, :].rearrange("p j (b th) -> p (j b) th", th=2),
+                    hs[:, ft, :, :].rearrange("p j (b th) -> p (j b) th", th=2),
+                    gr[:, ft, :, :].rearrange("p (th j) b -> p (j b) th", th=2),
+                )
+            ft0 = 2 * (n % 2)
+            minus_one_times(extra[:], hs[:, :, PACK - 1, :], tiles["g1_t", n // 2][:, ft0:ft0 + 2, :])
+            tiles["dct", n], tiles["extra", n] = dct, extra
+
+        def dc_back(n):
+            dct, extra = tiles["dct", n], tiles["extra", n]
+            ft0 = 2 * (n % 2)
+            banks = []
+            for jp in range(2):
+                bk = bank("dc", [P, 2, CW], F32)
+                for jj in range(2):
+                    j = 2 * jp + jj
+                    for ft in range(2):
+                        terms = [dct[:, ft, j, :]]
+                        if j == PACK - 1:
+                            terms = terms + [extra[:, ft, :], tiles["g2_neg_t", n // 2][:, ft0 + ft, :]]
+                        add_transposed(bk[:, jj, ft * P:(ft + 1) * P], terms)
+                banks.append(bk)
+            tiles["dc", n] = banks
+
+        def factors_ig(n):
+            b, sg, i = tiles["b", n], tiles["sg", n], tiles["i", n]
+            minus_one_times(b[:], i[:], b[:])
+            minus_one_times(sg[:], sg[:], i[:])
+            tiles["u", GATE_I, n], tiles["u", GATE_G, n] = b, sg
+
+        def factor_f(n):
+            f = tiles["f", n]
+            minus_one_times(f[:], f[:], tiles["a", n][:])
+            tiles["u", GATE_F, n] = f
+
+        def round_dz(n, gate):
+            if n % 2 == 0:
+                tiles["dz", gate, n // 2] = ring("dz%d_" % gate, 2, [P, PACK, K_PASS], BF16)
+            dz = tiles["dz", gate, n // 2]
+            cols = slice((n % 2) * CW, (n % 2 + 1) * CW)
+            for jp in range(2):
+                js = slice(2 * jp, 2 * jp + 2)
+                nc.vector.tensor_tensor(out=dz[:, js, cols], in0=tiles["dc", n][jp][:],
+                                        in1=tiles["u", gate, n][:, js, :], op=ALU.mult)
+
+        def group_tokens(n, gate, engine):
+            t = ring("tokg", 6, [P, CW, PACK], BF16)
+            cols = slice((n % 2) * CW, (n % 2 + 1) * CW)
+            interleave(engine, t[:], tiles["dz", gate, n // 2][:, :, cols])
+            tiles["tokg", gate, n] = t
+
+        def quantise_tokens(n, gate):
+            if ("tok", n) not in tiles:
+                tiles["tok", n] = (ring("tokc", 4, [P, 3, CW], U32), ring("toks", 4, [P, 3, CW], U8))
+            codes, scales = tiles["tok", n]
+            nc.vector.quantize_mx(out=codes[:, gate, :].bitcast(E5M2), scales=scales[:, gate, :],
+                                  in_=tiles["tokg", gate, n][:].rearrange("p w j -> p (w j)"))
+
+        def drain(bk, dst, engine):
+            stage = ring("stage", 10, [P, I], F32)
+            if engine == "scalar":
+                nc.scalar.copy(out=stage[:], in_=bk[:])
+            else:
+                nc.vector.tensor_copy(out=stage[:], in_=bk[:])
+            nc.sync.dma_start(out=dst, in_=stage[:])
+
+        def dw_tile(n, gate, m, engine, kind="mx"):
+            bk = bank(kind, [P, I], F32)
+            for g in range(2):
+                codes, scales = tiles["tok", n - 2 + 2 * g]
+                cols = slice(m * P, (m + 1) * P)
+                nc.tensor.matmul_mx(out=bk[:], lhsT=codes[:, gate, cols].bitcast(E5M2), lhsT_scale=scales[:, gate, cols],
+                                    rhs=op_codes[:, g, :].bitcast(E4M3), rhs_scale=op_scales[:, g, :],
+                                    start=(g == 0), stop=(g == 1))
+            r0 = col0(n) + m * P
+            drain(bk, dw_out[gate][r0:r0 + P, :], engine)
+
+        def turn_dz(q, gate):
+            words = tiles["dz", gate, q][:].rearrange("p j f -> p (j f)").bitcast(F32)
+            t = ring("grp", 3, [P, PACK * P * PACK], BF16)
+            t_words = t[:].bitcast(F32).rearrange("q (j p u) -> q j p u", j=PACK, u=2)
+            for jp in range(2):
+                bk = bank("tr", [P, 2, 2, P], F32)
+                for jj in range(2):
+                    w0 = (2 * jp + jj) * 256
+                    for u in range(2):
+                        nc.tensor.transpose(bk[:, jj, u, :], words[:, w0 + u:w0 + 256:2], ident[:])
+                nc.scalar.copy(out=t_words[:, 2 * jp:2 * jp + 2, :, :], in_=bk[:].rearrange("q j u p -> q j p u"))
+            tiles["featg", gate, q] = t
+
+        def quantise_features(q, gate):
+            codes = ring("featc", 9, [P, K_PASS], U32)
+            scales = ring("feats", 9, [P, K_PASS], U8)
+            nc.vector.quantize_mx(out=codes[:].bitcast(E5M2), scales=scales[:], in_=tiles["featg", gate, q][:])
+            tiles["feat", gate, q] = (codes, scales)
+
+        def dx_passes(g, j, h, gates, kind):
+            if ("dx", g, j) not in tiles:
+                tiles["dx", g, j] = bank(kind, [P, I], F32)
+            bk = tiles["dx", g, j]
+            for gate in gates:
+                codes, scales = tiles["feat", gate, 2 * h + g]
+                k = 2 + 3 * h + gate
+                cols = slice(j * P, (j + 1) * P)
+                nc.tensor.matmul_mx(out=bk[:], lhsT=codes[:, cols].bitcast(E5M2), lhsT_scale=scales[:, cols],
+                                    rhs=op_codes[:, k, :].bitcast(E4M3), rhs_scale=op_scales[:, k, :],
+                                    start=(h == 0 and gate == GATE_ORDER[0]), stop=(h == 1 and gate == GATE_ORDER[-1]))
+
+        def dx_drain(g, j, engine):
+            drain(tiles["dx", g, j], dx_rows[g, :, j, :], engine)
+
+        first, second, third = GATE_ORDER
+        load_ig(0)
+        load_f(0)
+        load_quarter(0)
+        load_grad(0)
+        nc.vector.memset(last_rows[:].rearrange("p g w -> p (g w)").bitcast(U32), 0)
+        make_identity(nc, ident[:])
+        make_identity(nc, ident_bf[:])
+        load_last_step(0)
+        load_f(1)
+        load_ig(1)
+        load_operand(0)
+        load_grad(1)
+        load_quarter(1)
+        load_f(2)
+        load_operand(1)
+
+        prod_b(0)
+        prod_a(0, nc.vector)
+        square_g(0)
+        cell_state(0)
+        tanh_c(0)
+        square_h(0)
+        turn_last_step(0)
+        factors_ig(0)
+        prod_a(1, nc.vector)
+
+        def dw_pair(n, gate):
+            for m in range(2):
+                dw_tile(n, gate, m, "scalar")
+
+        for n in range(CHUNKS - 1):
+            if n == 6:
+                turn_dz(2, first)
+            dc_turned(n)
+            if n % 2 == 0 and n < 6:
+                load_last_step(n // 2 + 1)
+            load_ig(n + 2)
+            load_f(n + 3)
+            load_grad(n + 2)
+            if n % 2 == 1:
+                load_quarter(n // 2 + 2)
+            if n <= 5:
+                load_operand(n + 2)
+            if n >= 1:
+                group_tokens(n - 1, first, "scalar")
+            dc_back(n)
+            prod_b(n + 1)
+            if n == 6:
+                turn_dz(2, second)
+            elif n >= 1:
+                group_tokens(n - 1, second, "scalar")
+            if n == 0:
+                group_operand(0, "scalar", 0, I)
+            cell_state(n + 1)
+            if n == 6:
+                turn_dz(2, third)
+            elif n >= 1:
+                group_tokens(n - 1, third, "scalar")
+            for k in {1: (0, 1), 2: (2, 3), 3: (4,), 4: (5,), 5: (6,), 6: (7,)}.get(n, ()):
+                quantise_operand(k)
+            if n in (3, 5):
+                for gate in GATE_ORDER:
+                    quantise_features({3: 0, 5: 1}[n], gate)
+            if n >= 1:
+                factors_ig(n)
+            tanh_c(n + 1)
+            if n == 6:
+                for gate in GATE_ORDER:
+                    quantise_features(2, gate)
+                for j in (0, 1):
+                    dx_passes(0, j, 1, GATE_ORDER, None)
+                for j in (2, 3):
+                    dx_passes(0, j, 0, GATE_ORDER, "ct")
+                    dx_passes(0, j, 1, GATE_ORDER, None)
+            elif n >= 1:
+                for gate in GATE_ORDER:
+                    quantise_tokens(n - 1, gate)
+            factor_f(n)
+            prod_a(n + 2, nc.gpsimd)
+            for gate in GATE_ORDER:
+                round_dz(n, gate)
+            steps = [lambda: square_h(n + 1), lambda: square_g(n + 1), lambda: None]
+            for gate, step in zip(GATE_ORDER, steps):
+                if n in (2, 4):
+                    turn_dz({2: 0, 4: 1}[n], gate)
+                if n in (3, 5):
+                    dw_pair({3: 2, 5: 3}[n], gate)
+                step()
+            if n % 2 == 1 and n < 6:
+                turn_last_step(n // 2 + 1)
+            if n == 0:
+                group_operand(1, "scalar", 0, I)
+            if n == 1:
+                group_operand(2, "scalar", 0, I)
+            if 1 <= n <= 5:
+                group_operand(n + 2, "vector", 0, SPLIT)
+                group_operand(n + 2, "scalar", SPLIT, I)
+            if n == 5:
+                for j in (0, 1):
+                    dx_passes(0, j, 0, GATE_ORDER, "mx")
+            if n == 6:
+                for j in range(PACK):
+                    dx_drain(0, j, "scalar")
+
+        n = CHUNKS - 1
+        dc_turned(n)
+        for gate in GATE_ORDER:
+            group_tokens(n - 1, gate, "scalar")
+        dc_back(n)
+        for j in (0, 1):
+            dx_passes(1, j, 0, GATE_ORDER, "ct")
+        quantise_tokens(n - 2, first)
+        factors_ig(n)
+        for gate in GATE_ORDER:
+            quantise_tokens(n - 1, gate)
+        factor_f(n)
+        dw_pair(n - 1, first)
+        group_tokens(n - 2, second, "scalar")
+        dw_pair(n - 1, second)
+        group_tokens(n - 2, third, "scalar")
+        dw_pair(n - 1, third)
+        round_dz(n, first)
+        turn_dz(3, first)
+        dx_passes(1, 2, 0, GATE_ORDER, "mx")
+        round_dz(n, second)
+        turn_dz(3, second)
+        dx_passes(1, 3, 0, GATE_ORDER, "mx")
+        round_dz(n, third)
+        turn_dz(3, third)
+        group_tokens(n, first, "vector")
+        quantise_tokens(n - 2, second)
+        quantise_tokens(n, first)
+        quantise_features(3, first)
+        group_tokens(n, second, "vector")
+        quantise_features(3, second)
+        quantise_tokens(n, second)
+        group_tokens(n, third, "scalar")
+        quantise_features(3, third)
+        quantise_tokens(n - 2, third)
+        quantise_tokens(n, third)
+        dw_tile(n, first, 0, "scalar", "dc")
+        dw_tile(n, first, 1, "scalar", "dc")
+        for j in range(PACK):
+            dx_passes(1, j, 1, [first, second], None)
+        for j in range(PACK):
+            dx_passes(1, j, 1, [third], None)
+            dx_drain(1, j, "vector" if j % 2 == 0 else "scalar")
+        dw_tile(n, second, 0, "vector", "tr")
+        dw_tile(n, second, 1, "scalar", "tr")
+        dw_tile(n, third, 0, "vector", "dc")
+        dw_tile(n, third, 1, "scalar", "dc")

@@ -22,7 +22,9 @@ PACK = 4
 K_PASS = P * PACK
 CW = 256
 CHUNKS = 8
-SPLIT = 256
+OPERAND_LOADS = {0: (2,), 1: (3,), 2: (4,), 3: (5,), 4: (6, 7)}
+OPERAND_GROUP = {0: ((1, 0, 0),), 1: ((2, 128, 0),), 2: ((3, 128, 0),), 3: ((4, 128, 256),), 4: ((5, 128, 256),), 5: ((6, 128, 128), (7, 0, 256))}
+OPERAND_QUANT = {1: (0, 1), 2: (2,), 3: (3,), 4: (4,), 5: (5,), 6: (6, 7)}
 GATE_F, GATE_I, GATE_G = 0, 1, 2
 GATE_ORDER = (GATE_I, GATE_G, GATE_F)
 
@@ -73,19 +75,19 @@ def tile_lstm_cell_pa_v_kernel(
 
         tiles = {}
 
-        def load_saved(kind, slots, n):
+        def load_saved(kind, slots, n, lo=0, hi=CW):
             if n >= CHUNKS:
                 return
-            t = ring("in_" + kind, slots, [P, PACK, CW], F32)
-            nc.sync.dma_start(out=t[:], in_=saved[kind][tpass(n), :, :, col0(n):col0(n) + CW])
-            tiles[kind, n] = t
+            if lo == 0:
+                tiles[kind, n] = ring("in_" + kind, slots, [P, PACK, CW], F32)
+            nc.sync.dma_start(out=tiles[kind, n][:, :, lo:hi], in_=saved[kind][tpass(n), :, :, col0(n) + lo:col0(n) + hi])
 
-        def load_f(n):
-            load_saved("f", 4, n)
+        def load_f(n, lo=0, hi=CW):
+            load_saved("f", 4, n, lo, hi)
 
-        def load_ig(n):
-            load_saved("i", 3, n)
-            load_saved("g", 2, n)
+        def load_ig(n, lo=0, hi=CW):
+            load_saved("i", 3, n, lo, hi)
+            load_saved("g", 2, n, lo, hi)
 
         def load_grad(n):
             if n >= CHUNKS:
@@ -115,11 +117,14 @@ def tile_lstm_cell_pa_v_kernel(
         def load_operand(k):
             t = ring("raw", 3, [P, PACK, I], BF16)
             if k < 2:
-                src = x_rows[k]
+                nc.sync.dma_start(out=t[:], in_=x_rows[k])
             else:
-                h, gate = divmod(k - 2, 3)
-                src = weights[gate][h * K_PASS:(h + 1) * K_PASS, :].rearrange("(p j) w -> p j w", j=PACK)
-            nc.sync.dma_start(out=t[:], in_=src)
+                h, s = divmod(k - 2, 3)
+                for side in range(2):
+                    c2, place = divmod(2 * s + side, 3)
+                    r0 = h * K_PASS + c2 * CW
+                    src = weights[GATE_ORDER[place]][r0:r0 + CW, :].rearrange("(p j) w -> p j w", j=PACK)
+                    nc.sync.dma_start(out=t[64 * side:64 * (side + 1), :, :], in_=src)
             tiles["raw", k] = t
 
         def interleave(engine, dst, src):
@@ -127,8 +132,11 @@ def tile_lstm_cell_pa_v_kernel(
             s = src.rearrange("p j (c i) -> p c j i", i=4)
             if engine == "scalar":
                 nc.scalar.copy(out=d, in_=s)
-            else:
+            elif engine == "vector":
                 nc.vector.tensor_copy(out=d, in_=s)
+            else:
+                nc.gpsimd.tensor_scalar(out=dst, in0=src.rearrange("p j w -> p w j"), scalar1=1.0, scalar2=0.0,
+                                        op0=ALU.mult, op1=ALU.add)
 
         def group_operand(k, engine, lo, hi):
             if ("grouped", k) not in tiles:
@@ -160,22 +168,29 @@ def tile_lstm_cell_pa_v_kernel(
             nc.scalar.activation(out=g2_neg_t[:], in_=bk[:, 1, :, :], func=ACT.Copy, scale=-1.0)
             tiles["g1_t", q], tiles["g2_neg_t", q] = g1_t, g2_neg_t
 
-        def prod_a(n, engine):
+        def prod_a(n, engine, lo=0, hi=CW):
             if n >= CHUNKS:
                 return
-            a = ring("a", 2, [P, PACK, CW], F32)
-            c0_b = tiles["c0", n // 2][:, (n % 2) * CW:(n % 2 + 1) * CW].unsqueeze(1).to_broadcast([P, PACK, CW])
-            engine.tensor_tensor(out=a[:], in0=tiles["f", n][:], in1=c0_b, op=ALU.mult)
-            tiles["a", n] = a
+            if lo == 0:
+                tiles["a", n] = ring("a", 2, [P, PACK, CW], F32)
+            c_lo = (n % 2) * CW
+            c0_b = tiles["c0", n // 2][:, c_lo + lo:c_lo + hi].unsqueeze(1).to_broadcast([P, PACK, hi - lo])
+            engine.tensor_tensor(out=tiles["a", n][:, :, lo:hi], in0=tiles["f", n][:, :, lo:hi], in1=c0_b, op=ALU.mult)
 
-        def prod_b(n):
-            b = ring("b", 2, [P, PACK, CW], F32)
-            nc.vector.tensor_tensor(out=b[:], in0=tiles["i", n][:], in1=tiles["g", n][:], op=ALU.mult)
-            tiles["b", n] = b
+        def prod_b(n, lo=0, hi=CW):
+            if lo == 0:
+                tiles["b", n] = ring("b", 2, [P, PACK, CW], F32)
+            nc.vector.tensor_tensor(out=tiles["b", n][:, :, lo:hi], in0=tiles["i", n][:, :, lo:hi],
+                                    in1=tiles["g", n][:, :, lo:hi], op=ALU.mult)
 
         def square_g(n):
-            sg = ring("sg", 2, [P, PACK, CW], F32)
-            nc.scalar.activation(out=sg[:], in_=tiles["g", n][:], func=ACT.Square)
+            g = tiles["g", n]
+            if n == CHUNKS - 1:
+                sg = ring("a", 2, [P, PACK, CW], F32)
+                nc.gpsimd.tensor_tensor(out=sg[:], in0=g[:], in1=g[:], op=ALU.mult)
+            else:
+                sg = ring("sg", 2, [P, PACK, CW], F32)
+                nc.scalar.activation(out=sg[:], in_=g[:], func=ACT.Square)
             tiles["sg", n] = sg
 
         def add_transposed(out, terms):
@@ -183,25 +198,23 @@ def tile_lstm_cell_pa_v_kernel(
                 nc.tensor.matmul(out, lhsT=term, rhs=ident[:], is_transpose=True,
                                  start=(k == 0), stop=(k == len(terms) - 1))
 
-        def cell_state(n):
-            banks = []
-            for ft in range(2):
+        def cell_state(n, fts=(0, 1)):
+            for ft in fts:
                 bk = bank("ct", [P, PACK, P], F32)
                 for j in range(PACK):
                     cols = slice(ft * P, (ft + 1) * P)
                     add_transposed(bk[:, j, :], [tiles["a", n][:, j, cols], tiles["b", n][:, j, cols]])
-                banks.append(bk)
-            tiles["ct", n] = banks
+                tiles["ct", n, ft] = bk
 
-        def tanh_c(n):
-            hs = ring("hs", 1, [P, 2, PACK, P], F32)
-            for ft in range(2):
-                nc.scalar.activation(out=hs[:, ft, :, :], in_=tiles["ct", n][ft][:], func=ACT.Tanh)
-            tiles["hs", n] = hs
+        def tanh_c(n, fts=(0, 1)):
+            for ft in fts:
+                if ft == 0:
+                    tiles["hs", n] = ring("hs", 1, [P, 2, PACK, P], F32)
+                nc.scalar.activation(out=tiles["hs", n][:, ft, :, :], in_=tiles["ct", n, ft][:], func=ACT.Tanh)
 
-        def square_h(n):
-            hs = tiles["hs", n]
-            nc.scalar.activation(out=hs[:], in_=hs[:], func=ACT.Square)
+        def square_h(n, lo=0, hi=2):
+            hs = tiles["hs", n][:, lo:hi, :, :]
+            nc.scalar.activation(out=hs, in_=hs, func=ACT.Square)
 
         def minus_one_times(out, in0, in1):
             nc.vector.scalar_tensor_tensor(out=out, in0=in0, scalar=1.0, in1=in1, op0=ALU.subtract, op1=ALU.mult)
@@ -236,31 +249,37 @@ def tile_lstm_cell_pa_v_kernel(
                 banks.append(bk)
             tiles["dc", n] = banks
 
-        def factors_ig(n):
-            b, sg, i = tiles["b", n], tiles["sg", n], tiles["i", n]
-            minus_one_times(b[:], i[:], b[:])
-            minus_one_times(sg[:], sg[:], i[:])
-            tiles["u", GATE_I, n], tiles["u", GATE_G, n] = b, sg
+        def factor_i(n):
+            b = tiles["b", n]
+            minus_one_times(b[:], tiles["i", n][:], b[:])
+            tiles["u", GATE_I, n] = b
+
+        def factor_g(n):
+            sg = tiles["sg", n]
+            minus_one_times(sg[:], sg[:], tiles["i", n][:])
+            tiles["u", GATE_G, n] = sg
 
         def factor_f(n):
             f = tiles["f", n]
             minus_one_times(f[:], f[:], tiles["a", n][:])
             tiles["u", GATE_F, n] = f
 
+        def dz_view(n, gate):
+            s, side = divmod(3 * (n % 2) + GATE_ORDER.index(gate), 2)
+            if ("dz", n // 2, s) not in tiles:
+                tiles["dz", n // 2, s] = ring("dz", 6, [P, PACK, K_PASS], BF16)
+            return tiles["dz", n // 2, s][:, :, side * CW:(side + 1) * CW]
+
         def round_dz(n, gate):
-            if n % 2 == 0:
-                tiles["dz", gate, n // 2] = ring("dz%d_" % gate, 2, [P, PACK, K_PASS], BF16)
-            dz = tiles["dz", gate, n // 2]
-            cols = slice((n % 2) * CW, (n % 2 + 1) * CW)
+            dz = dz_view(n, gate)
             for jp in range(2):
                 js = slice(2 * jp, 2 * jp + 2)
-                nc.vector.tensor_tensor(out=dz[:, js, cols], in0=tiles["dc", n][jp][:],
+                nc.vector.tensor_tensor(out=dz[:, js, :], in0=tiles["dc", n][jp][:],
                                         in1=tiles["u", gate, n][:, js, :], op=ALU.mult)
 
         def group_tokens(n, gate, engine):
-            t = ring("tokg", 6, [P, CW, PACK], BF16)
-            cols = slice((n % 2) * CW, (n % 2 + 1) * CW)
-            interleave(engine, t[:], tiles["dz", gate, n // 2][:, :, cols])
+            t = ring("tokg", 4, [P, CW, PACK], BF16)
+            interleave(engine, t[:], dz_view(n, gate))
             tiles["tokg", gate, n] = t
 
         def quantise_tokens(n, gate):
@@ -271,7 +290,7 @@ def tile_lstm_cell_pa_v_kernel(
                                   in_=tiles["tokg", gate, n][:].rearrange("p w j -> p (w j)"))
 
         def drain(bk, dst, engine):
-            stage = ring("stage", 10, [P, I], F32)
+            stage = ring("stage", 8, [P, I], F32)
             if engine == "scalar":
                 nc.scalar.copy(out=stage[:], in_=bk[:])
             else:
@@ -289,8 +308,8 @@ def tile_lstm_cell_pa_v_kernel(
             r0 = col0(n) + m * P
             drain(bk, dw_out[gate][r0:r0 + P, :], engine)
 
-        def turn_dz(q, gate):
-            words = tiles["dz", gate, q][:].rearrange("p j f -> p (j f)").bitcast(F32)
+        def turn_dz(q, s):
+            words = tiles["dz", q, s][:].rearrange("p j f -> p (j f)").bitcast(F32)
             t = ring("grp", 3, [P, PACK * P * PACK], BF16)
             t_words = t[:].bitcast(F32).rearrange("q (j p u) -> q j p u", j=PACK, u=2)
             for jp in range(2):
@@ -300,178 +319,197 @@ def tile_lstm_cell_pa_v_kernel(
                     for u in range(2):
                         nc.tensor.transpose(bk[:, jj, u, :], words[:, w0 + u:w0 + 256:2], ident[:])
                 nc.scalar.copy(out=t_words[:, 2 * jp:2 * jp + 2, :, :], in_=bk[:].rearrange("q j u p -> q j p u"))
-            tiles["featg", gate, q] = t
+            tiles["featg", q, s] = t
 
-        def quantise_features(q, gate):
+        def quantise_features(q, s):
             codes = ring("featc", 9, [P, K_PASS], U32)
             scales = ring("feats", 9, [P, K_PASS], U8)
-            nc.vector.quantize_mx(out=codes[:].bitcast(E5M2), scales=scales[:], in_=tiles["featg", gate, q][:])
-            tiles["feat", gate, q] = (codes, scales)
+            nc.vector.quantize_mx(out=codes[:].bitcast(E5M2), scales=scales[:], in_=tiles["featg", q, s][:])
+            tiles["feat", q, s] = (codes, scales)
 
-        def dx_passes(g, j, h, gates, kind):
-            if ("dx", g, j) not in tiles:
-                tiles["dx", g, j] = bank(kind, [P, I], F32)
-            bk = tiles["dx", g, j]
-            for gate in gates:
-                codes, scales = tiles["feat", gate, 2 * h + g]
-                k = 2 + 3 * h + gate
+        def dx_passes(key, g, j, passes, kind, opens, closes):
+            if opens:
+                tiles["dx", key, j] = bank(kind, [P, I], F32)
+            bk = tiles["dx", key, j]
+            for idx, k in enumerate(passes):
+                h, s = divmod(k, 3)
+                codes, scales = tiles["feat", 2 * h + g, s]
                 cols = slice(j * P, (j + 1) * P)
                 nc.tensor.matmul_mx(out=bk[:], lhsT=codes[:, cols].bitcast(E5M2), lhsT_scale=scales[:, cols],
-                                    rhs=op_codes[:, k, :].bitcast(E4M3), rhs_scale=op_scales[:, k, :],
-                                    start=(h == 0 and gate == GATE_ORDER[0]), stop=(h == 1 and gate == GATE_ORDER[-1]))
+                                    rhs=op_codes[:, 2 + k, :].bitcast(E4M3), rhs_scale=op_scales[:, 2 + k, :],
+                                    start=(opens and idx == 0), stop=(closes and idx == len(passes) - 1))
 
-        def dx_drain(g, j, engine):
-            drain(tiles["dx", g, j], dx_rows[g, :, j, :], engine)
+        def dx_drain(j):
+            drain(tiles["dx", "g0", j], dx_rows[0, :, j, :], "scalar")
+
+        dx_part = sb.tile([P, PACK, I], F32, name="dx_part", align_bytes=64)
+
+        def dx_park(j):
+            dx_passes("park", 1, j, (0, 1, 2), "mx", True, True)
+            nc.scalar.copy(out=dx_part[:, j, :], in_=tiles["dx", "park", j][:])
+
+        def dx_finish(j):
+            nc.vector.tensor_tensor(out=dx_part[:, j, :], in0=tiles["dx", "g1", j][:], in1=dx_part[:, j, :], op=ALU.add)
+            nc.sync.dma_start(out=dx_rows[1, :, j, :], in_=dx_part[:, j, :])
 
         first, second, third = GATE_ORDER
-        load_ig(0)
-        load_f(0)
+        load_ig(0, 0, P)
+        load_f(0, 0, P)
         load_quarter(0)
+        load_ig(0, P, CW)
+        load_f(0, P, CW)
         load_grad(0)
         nc.vector.memset(last_rows[:].rearrange("p g w -> p (g w)").bitcast(U32), 0)
         make_identity(nc, ident[:])
         make_identity(nc, ident_bf[:])
         load_last_step(0)
+        load_operand(0)
         load_f(1)
         load_ig(1)
-        load_operand(0)
-        load_grad(1)
         load_quarter(1)
         load_f(2)
+        load_grad(1)
         load_operand(1)
 
-        prod_b(0)
-        prod_a(0, nc.vector)
-        square_g(0)
-        cell_state(0)
-        tanh_c(0)
-        square_h(0)
+        for ft in range(2):
+            prod_b(0, ft * P, (ft + 1) * P)
+            prod_a(0, nc.vector, ft * P, (ft + 1) * P)
+            cell_state(0, (ft,))
+            tanh_c(0, (ft,))
+            square_h(0, ft, ft + 1)
+            if ft == 0:
+                square_g(0)
         turn_last_step(0)
-        factors_ig(0)
-        prod_a(1, nc.vector)
+        factor_i(0)
+        factor_g(0)
+        load_ig(2)
+        group_operand(0, "scalar", 0, I)
 
         def dw_pair(n, gate):
             for m in range(2):
                 dw_tile(n, gate, m, "scalar")
 
+        def ready_passes(n):
+            if n < 0:
+                return []
+            return [(n // 2, s) for s in ((0,) if n % 2 == 0 else (1, 2))]
+
         for n in range(CHUNKS - 1):
-            if n == 6:
-                turn_dz(2, first)
+            turns = ready_passes(n - 1)
             dc_turned(n)
+            if n > 0:
+                load_ig(n + 2)
             if n % 2 == 0 and n < 6:
                 load_last_step(n // 2 + 1)
-            load_ig(n + 2)
-            load_f(n + 3)
             load_grad(n + 2)
+            load_f(n + 3)
             if n % 2 == 1:
                 load_quarter(n // 2 + 2)
-            if n <= 5:
-                load_operand(n + 2)
+            for k in OPERAND_LOADS.get(n, ()):
+                load_operand(k)
+            if n == 6:
+                turn_dz(*turns[0])
             if n >= 1:
                 group_tokens(n - 1, first, "scalar")
             dc_back(n)
+            if n == 0:
+                prod_a(1, nc.vector)
+                factor_f(0)
             prod_b(n + 1)
             if n == 6:
-                turn_dz(2, second)
-            elif n >= 1:
-                group_tokens(n - 1, second, "scalar")
-            if n == 0:
-                group_operand(0, "scalar", 0, I)
-            cell_state(n + 1)
-            if n == 6:
-                turn_dz(2, third)
-            elif n >= 1:
-                group_tokens(n - 1, third, "scalar")
-            for k in {1: (0, 1), 2: (2, 3), 3: (4,), 4: (5,), 5: (6,), 6: (7,)}.get(n, ()):
-                quantise_operand(k)
-            if n in (3, 5):
-                for gate in GATE_ORDER:
-                    quantise_features({3: 0, 5: 1}[n], gate)
+                turn_dz(*turns[1])
             if n >= 1:
-                factors_ig(n)
+                group_tokens(n - 1, second, "scalar")
+            cell_state(n + 1)
+            if n >= 1:
+                group_tokens(n - 1, third, "scalar")
+            for q, s in ready_passes(n - 2):
+                quantise_features(q, s)
+            if n >= 1:
+                factor_i(n)
+                factor_g(n)
+            for k in OPERAND_QUANT.get(n, ()):
+                quantise_operand(k)
             tanh_c(n + 1)
             if n == 6:
-                for gate in GATE_ORDER:
-                    quantise_features(2, gate)
+                for q, s in turns:
+                    quantise_features(q, s)
                 for j in (0, 1):
-                    dx_passes(0, j, 1, GATE_ORDER, None)
+                    dx_passes("g0", 0, j, (3, 4, 5), None, False, True)
                 for j in (2, 3):
-                    dx_passes(0, j, 0, GATE_ORDER, "ct")
-                    dx_passes(0, j, 1, GATE_ORDER, None)
-            elif n >= 1:
+                    dx_passes("g0", 0, j, range(6), "ct", True, True)
+            if n >= 1:
                 for gate in GATE_ORDER:
                     quantise_tokens(n - 1, gate)
-            factor_f(n)
+            if n >= 1:
+                factor_f(n)
             prod_a(n + 2, nc.gpsimd)
+            for k, to_pool, to_vector in OPERAND_GROUP.get(n, ()):
+                group_operand(k, "gpsimd", 0, to_pool)
             for gate in GATE_ORDER:
                 round_dz(n, gate)
             steps = [lambda: square_h(n + 1), lambda: square_g(n + 1), lambda: None]
-            for gate, step in zip(GATE_ORDER, steps):
-                if n in (2, 4):
-                    turn_dz({2: 0, 4: 1}[n], gate)
-                if n in (3, 5):
-                    dw_pair({3: 2, 5: 3}[n], gate)
+            for place, step in enumerate(steps):
+                if n != 6 and place < len(turns):
+                    turn_dz(*turns[place])
                 step()
+                if n in (3, 4):
+                    dw_pair(n - 1, GATE_ORDER[place])
+                if n == 5 and place < 2:
+                    for j in (2 * place, 2 * place + 1):
+                        dx_park(j)
             if n % 2 == 1 and n < 6:
                 turn_last_step(n // 2 + 1)
-            if n == 0:
-                group_operand(1, "scalar", 0, I)
-            if n == 1:
-                group_operand(2, "scalar", 0, I)
-            if 1 <= n <= 5:
-                group_operand(n + 2, "vector", 0, SPLIT)
-                group_operand(n + 2, "scalar", SPLIT, I)
+            for k, to_pool, to_vector in OPERAND_GROUP.get(n, ()):
+                group_operand(k, "vector", to_pool, to_pool + to_vector)
+                group_operand(k, "scalar", to_pool + to_vector, I)
             if n == 5:
                 for j in (0, 1):
-                    dx_passes(0, j, 0, GATE_ORDER, "mx")
+                    dx_passes("g0", 0, j, (0, 1, 2), "mx", True, False)
             if n == 6:
                 for j in range(PACK):
-                    dx_drain(0, j, "scalar")
+                    dx_drain(j)
 
         n = CHUNKS - 1
         dc_turned(n)
         for gate in GATE_ORDER:
             group_tokens(n - 1, gate, "scalar")
         dc_back(n)
-        for j in (0, 1):
-            dx_passes(1, j, 0, GATE_ORDER, "ct")
-        quantise_tokens(n - 2, first)
-        factors_ig(n)
+        turn_dz(3, 0)
+        factor_i(n)
+        factor_g(n)
         for gate in GATE_ORDER:
             quantise_tokens(n - 1, gate)
         factor_f(n)
-        dw_pair(n - 1, first)
-        group_tokens(n - 2, second, "scalar")
-        dw_pair(n - 1, second)
-        group_tokens(n - 2, third, "scalar")
-        dw_pair(n - 1, third)
+        quantise_features(3, 0)
+        for place, gate in enumerate(GATE_ORDER):
+            for m in range(2):
+                dw_tile(n - 1, gate, m, "scalar", "ct" if place == 1 else "mx")
         round_dz(n, first)
-        turn_dz(3, first)
-        dx_passes(1, 2, 0, GATE_ORDER, "mx")
+        for j in (0, 1):
+            dx_passes("g1", 1, j, (3,), "ct", True, False)
+        turn_dz(3, 1)
+        for j in (2, 3):
+            dx_passes("g1", 1, j, (3,), "mx", True, False)
+        group_tokens(n, first, "scalar")
         round_dz(n, second)
-        turn_dz(3, second)
-        dx_passes(1, 3, 0, GATE_ORDER, "mx")
         round_dz(n, third)
-        turn_dz(3, third)
-        group_tokens(n, first, "vector")
-        quantise_tokens(n - 2, second)
-        quantise_tokens(n, first)
-        quantise_features(3, first)
+        turn_dz(3, 2)
+        quantise_features(3, 1)
         group_tokens(n, second, "vector")
-        quantise_features(3, second)
+        quantise_tokens(n, first)
+        group_tokens(n, third, "vector")
         quantise_tokens(n, second)
-        group_tokens(n, third, "scalar")
-        quantise_features(3, third)
-        quantise_tokens(n - 2, third)
+        quantise_features(3, 2)
         quantise_tokens(n, third)
+        for j in range(PACK):
+            dx_passes("g1", 1, j, (4,), None, False, False)
         dw_tile(n, first, 0, "scalar", "dc")
         dw_tile(n, first, 1, "scalar", "dc")
-        for j in range(PACK):
-            dx_passes(1, j, 1, [first, second], None)
-        for j in range(PACK):
-            dx_passes(1, j, 1, [third], None)
-            dx_drain(1, j, "vector" if j % 2 == 0 else "scalar")
-        dw_tile(n, second, 0, "vector", "tr")
+        dw_tile(n, second, 0, "scalar", "tr")
         dw_tile(n, second, 1, "scalar", "tr")
-        dw_tile(n, third, 0, "vector", "dc")
+        for j in range(PACK):
+            dx_passes("g1", 1, j, (5,), None, False, True)
+            dx_finish(j)
+        dw_tile(n, third, 0, "scalar", "dc")
         dw_tile(n, third, 1, "scalar", "dc")

@@ -23,7 +23,7 @@ K_PASS = P * PACK
 CW = 256
 CHUNKS = 8
 OPERAND_LOADS = {0: (2,), 1: (3,), 2: (4,), 3: (5,), 4: (6, 7)}
-OPERAND_GROUP = {0: ((1, 0, 0),), 1: ((2, 128, 0),), 2: ((3, 128, 0),), 3: ((4, 128, 256),), 4: ((5, 128, 256),), 5: ((6, 128, 128), (7, 0, 256))}
+OPERAND_GROUP = {0: ((1, 0, 0),), 1: ((2, 0, 0),), 2: ((3, 0, 128),), 3: ((4, 0, 512),), 4: ((5, 0, 512),), 5: ((6, 0, 256), (7, 0, 384))}
 OPERAND_QUANT = {1: (0, 1), 2: (2,), 3: (3,), 4: (4,), 5: (5,), 6: (6, 7)}
 GATE_F, GATE_I, GATE_G = 0, 1, 2
 GATE_ORDER = (GATE_I, GATE_G, GATE_F)
@@ -278,16 +278,17 @@ def tile_lstm_cell_pa_v_kernel(
                                         in1=tiles["u", gate, n][:, js, :], op=ALU.mult)
 
         def group_tokens(n, gate, engine):
-            t = ring("tokg", 4, [P, CW, PACK], BF16)
-            interleave(engine, t[:], dz_view(n, gate))
-            tiles["tokg", gate, n] = t
+            if ("tokg", n) not in tiles:
+                tiles["tokg", n] = ring("tokg", 2, [P, 3, CW, PACK], BF16)
+            interleave(engine, tiles["tokg", n][:, GATE_ORDER.index(gate), :, :], dz_view(n, gate))
 
-        def quantise_tokens(n, gate):
+        def quantise_tokens(n, lo, hi):
             if ("tok", n) not in tiles:
                 tiles["tok", n] = (ring("tokc", 4, [P, 3, CW], U32), ring("toks", 4, [P, 3, CW], U8))
             codes, scales = tiles["tok", n]
-            nc.vector.quantize_mx(out=codes[:, gate, :].bitcast(E5M2), scales=scales[:, gate, :],
-                                  in_=tiles["tokg", gate, n][:].rearrange("p w j -> p (w j)"))
+            nc.vector.quantize_mx(out=codes[:, lo:hi, :].rearrange("p k w -> p (k w)").bitcast(E5M2),
+                                  scales=scales[:, lo:hi, :].rearrange("p k w -> p (k w)"),
+                                  in_=tiles["tokg", n][:, lo:hi, :, :].rearrange("p k w j -> p (k w j)"))
 
         def drain(bk, dst, engine):
             stage = ring("stage", 8, [P, I], F32)
@@ -299,10 +300,11 @@ def tile_lstm_cell_pa_v_kernel(
 
         def dw_tile(n, gate, m, engine, kind="mx"):
             bk = bank(kind, [P, I], F32)
+            place = GATE_ORDER.index(gate)
             for g in range(2):
                 codes, scales = tiles["tok", n - 2 + 2 * g]
                 cols = slice(m * P, (m + 1) * P)
-                nc.tensor.matmul_mx(out=bk[:], lhsT=codes[:, gate, cols].bitcast(E5M2), lhsT_scale=scales[:, gate, cols],
+                nc.tensor.matmul_mx(out=bk[:], lhsT=codes[:, place, cols].bitcast(E5M2), lhsT_scale=scales[:, place, cols],
                                     rhs=op_codes[:, g, :].bitcast(E4M3), rhs_scale=op_scales[:, g, :],
                                     start=(g == 0), stop=(g == 1))
             r0 = col0(n) + m * P
@@ -439,8 +441,8 @@ def tile_lstm_cell_pa_v_kernel(
                 for j in (2, 3):
                     dx_passes("g0", 0, j, range(6), "ct", True, True)
             if n >= 1:
-                for gate in GATE_ORDER:
-                    quantise_tokens(n - 1, gate)
+                quantise_tokens(n - 1, 0, 2)
+                quantise_tokens(n - 1, 2, 3)
             if n >= 1:
                 factor_f(n)
             prod_a(n + 2, nc.gpsimd)
@@ -478,8 +480,8 @@ def tile_lstm_cell_pa_v_kernel(
         turn_dz(3, 0)
         factor_i(n)
         factor_g(n)
-        for gate in GATE_ORDER:
-            quantise_tokens(n - 1, gate)
+        quantise_tokens(n - 1, 0, 2)
+        quantise_tokens(n - 1, 2, 3)
         factor_f(n)
         quantise_features(3, 0)
         for place, gate in enumerate(GATE_ORDER):
@@ -491,25 +493,23 @@ def tile_lstm_cell_pa_v_kernel(
         turn_dz(3, 1)
         for j in (2, 3):
             dx_passes("g1", 1, j, (3,), "mx", True, False)
-        group_tokens(n, first, "scalar")
         round_dz(n, second)
         round_dz(n, third)
         turn_dz(3, 2)
+        group_tokens(n, first, "vector")
         quantise_features(3, 1)
+        quantise_tokens(n, 0, 1)
         group_tokens(n, second, "vector")
-        quantise_tokens(n, first)
-        group_tokens(n, third, "vector")
-        quantise_tokens(n, second)
+        group_tokens(n, third, "scalar")
         quantise_features(3, 2)
-        quantise_tokens(n, third)
-        for j in range(PACK):
-            dx_passes("g1", 1, j, (4,), None, False, False)
+        quantise_tokens(n, 1, 2)
+        quantise_tokens(n, 2, 3)
         dw_tile(n, first, 0, "scalar", "dc")
         dw_tile(n, first, 1, "scalar", "dc")
+        for j in range(PACK):
+            dx_passes("g1", 1, j, (4, 5), None, False, True)
+            dx_finish(j)
         dw_tile(n, second, 0, "scalar", "tr")
         dw_tile(n, second, 1, "scalar", "tr")
-        for j in range(PACK):
-            dx_passes("g1", 1, j, (5,), None, False, True)
-            dx_finish(j)
         dw_tile(n, third, 0, "scalar", "dc")
-        dw_tile(n, third, 1, "scalar", "dc")
+        dw_tile(n, third, 1, "vector", "dc")

@@ -21,12 +21,19 @@ P = 128
 PACK = 4
 K_PASS = P * PACK
 CW = 256
+FT = CW // P
+ROWS = B // 2
 CHUNKS = 8
-OPERAND_LOADS = {0: (2,), 1: (3,), 2: (4,), 3: (5,), 4: (6, 7)}
-OPERAND_GROUP = {0: ((1, 0, 0),), 1: ((2, 0, 0),), 2: ((3, 0, 128),), 3: ((4, 0, 512),), 4: ((5, 0, 512),), 5: ((6, 0, 256), (7, 0, 384))}
-OPERAND_QUANT = {1: (0, 1), 2: (2,), 3: (3,), 4: (4,), 5: (5,), 6: (6, 7)}
+QUARTERS = CHUNKS // 2
+LAST = CHUNKS - 1
 GATE_F, GATE_I, GATE_G = 0, 1, 2
-GATE_ORDER = (GATE_I, GATE_G, GATE_F)
+GATE_ORDER = (GATE_I, GATE_F, GATE_G)
+OPERANDS = 8
+
+DW_PERIODS = (3, 4)
+PARK_PERIOD = 5
+DX0_PERIOD = 6
+POOL_COLS = 128
 
 
 def tile_lstm_cell_pa_v_kernel(
@@ -36,51 +43,58 @@ def tile_lstm_cell_pa_v_kernel(
     nc = tc.nc
     weights = (W_f, W_i, W_g)
     dw_out = (out_1, out_2, out_3)
+    first, second, third = GATE_ORDER
 
-    def by_pass(ap):
+    def by_token_pass(ap):
         return ap.rearrange("b t w -> (b t) w").rearrange("(g p j) w -> g p j w", g=2, j=PACK)
 
-    saved = {"f": by_pass(f_t), "i": by_pass(i_t), "g": by_pass(g_t)}
-    x_rows = by_pass(x)
-    dx_rows = by_pass(out_0)
+    saved = {"f": by_token_pass(f_t), "i": by_token_pass(i_t), "g": by_token_pass(g_t)}
+    x_rows = by_token_pass(x)
+    dx_rows = by_token_pass(out_0)
     grad_cols = grad_0.rearrange("f (t g b) -> f t g b", t=T, g=2)
+
+    def token_pass(n):
+        return (n // 2) % 2
+
+    def first_feature(n):
+        return (n // 4) * K_PASS + (n % 2) * CW
+
+    def passes_completed_by(n):
+        if n < 0:
+            return []
+        return [(n // 2, s) for s in ((0,) if n % 2 == 0 else (1, 2))]
+
+    def operands_at(n, lead, latest):
+        return [k for k in range(OPERANDS) if min(k - lead, latest) == n]
 
     with ExitStack() as ctx:
         sb = ctx.enter_context(tc.tile_pool(name="sb", bufs=1))
         ps = ctx.enter_context(tc.psum_pool(name="ps", bufs=1))
         ctx.enter_context(tc.manual_schedule())
 
-        counters = {}
+        tiles = {}
+        handed_out = {}
+
+        def next_tag(kind, slots):
+            count = handed_out.get(kind, 0)
+            handed_out[kind] = count + 1
+            return "%s%d" % (kind, count % slots)
 
         def ring(kind, slots, shape, dtype):
-            k = counters.get(kind, 0)
-            counters[kind] = k + 1
-            tag = "%s%d" % (kind, k % slots)
+            tag = next_tag(kind, slots)
             return sb.tile(shape, dtype, name=tag, tag=tag, align_bytes=64)
 
         def bank(kind, shape, dtype):
-            k = counters.get(kind, 0)
-            counters[kind] = k + 1
-            tag = "%s%d" % (kind, k % 2)
+            tag = next_tag(kind, 2)
             return ps.tile(shape, dtype, name=tag, tag=tag)
 
-        def half(n):
-            return n // 4
-
-        def tpass(n):
-            return (n // 2) % 2
-
-        def col0(n):
-            return (2 * half(n) + n % 2) * CW
-
-        tiles = {}
-
-        def load_saved(kind, slots, n, lo=0, hi=CW):
+        def load_saved(kind, slots, n, lo, hi):
             if n >= CHUNKS:
                 return
             if lo == 0:
                 tiles[kind, n] = ring("in_" + kind, slots, [P, PACK, CW], F32)
-            nc.sync.dma_start(out=tiles[kind, n][:, :, lo:hi], in_=saved[kind][tpass(n), :, :, col0(n) + lo:col0(n) + hi])
+            f0 = first_feature(n)
+            nc.sync.dma_start(out=tiles[kind, n][:, :, lo:hi], in_=saved[kind][token_pass(n), :, :, f0 + lo:f0 + hi])
 
         def load_f(n, lo=0, hi=CW):
             load_saved("f", 4, n, lo, hi)
@@ -92,51 +106,54 @@ def tile_lstm_cell_pa_v_kernel(
         def load_grad(n):
             if n >= CHUNKS:
                 return
-            t = ring("grad", 3, [P, 2, T, B // 2], BF16)
-            for ft in range(2):
-                r0 = col0(n) + ft * P
-                nc.sync.dma_start(out=t[:, ft, :, :], in_=grad_cols[r0:r0 + P, :, tpass(n), :])
-            tiles["grad", n] = t
+            grad = ring("grad", 3, [P, FT, T, ROWS], BF16)
+            for ft in range(FT):
+                f0 = first_feature(n) + ft * P
+                nc.sync.dma_start(out=grad[:, ft, :, :], in_=grad_cols[f0:f0 + P, :, token_pass(n), :])
+            tiles["grad", n] = grad
 
-        def load_quarter(q):
-            if q >= 4:
+        def quarter_slices(q):
+            half, g = divmod(q, 2)
+            return slice(ROWS * g, ROWS * (g + 1)), slice(half * K_PASS, (half + 1) * K_PASS)
+
+        def load_c0(q):
+            if q >= QUARTERS:
                 return
-            h, g = divmod(q, 2)
-            rows, cols = slice(64 * g, 64 * (g + 1)), slice(h * K_PASS, (h + 1) * K_PASS)
-            t = ring("c0_", 2, [P, K_PASS], BF16)
+            rows, cols = quarter_slices(q)
+            c0_rows = ring("c0_", 2, [P, K_PASS], BF16)
             for th in range(2):
-                nc.sync.dma_start(out=t[th:P:2, :], in_=c0[rows, cols])
-            tiles["c0", q] = t
+                nc.sync.dma_start(out=c0_rows[th:P:2, :], in_=c0[rows, cols])
+            tiles["c0", q] = c0_rows
 
         def load_last_step(q):
-            h, g = divmod(q, 2)
-            rows, cols = slice(64 * g, 64 * (g + 1)), slice(h * K_PASS, (h + 1) * K_PASS)
+            rows, cols = quarter_slices(q)
             for k, src in enumerate((grad_1, grad_2)):
                 nc.sync.dma_start(out=last_rows[1:P:2, k, :], in_=src[rows, cols])
 
         def load_operand(k):
-            t = ring("raw", 3, [P, PACK, I], BF16)
+            raw = ring("raw", 3, [P, PACK, I], BF16)
             if k < 2:
-                nc.sync.dma_start(out=t[:], in_=x_rows[k])
+                nc.sync.dma_start(out=raw[:], in_=x_rows[k])
             else:
-                h, s = divmod(k - 2, 3)
+                half, s = divmod(k - 2, 3)
                 for side in range(2):
-                    c2, place = divmod(2 * s + side, 3)
-                    r0 = h * K_PASS + c2 * CW
-                    src = weights[GATE_ORDER[place]][r0:r0 + CW, :].rearrange("(p j) w -> p j w", j=PACK)
-                    nc.sync.dma_start(out=t[64 * side:64 * (side + 1), :, :], in_=src)
-            tiles["raw", k] = t
+                    chunk, place = divmod(2 * s + side, 3)
+                    r0 = half * K_PASS + chunk * CW
+                    src = weights[GATE_ORDER[place]][r0:r0 + CW, :].rearrange("(q r) w -> q r w", r=PACK)
+                    nc.sync.dma_start(out=raw[side * P // 2:(side + 1) * P // 2, :, :], in_=src)
+            tiles["raw", k] = raw
 
         def interleave(engine, dst, src):
-            d = dst.rearrange("p (c i) j -> p c j i", i=4)
-            s = src.rearrange("p j (c i) -> p c j i", i=4)
-            if engine == "scalar":
-                nc.scalar.copy(out=d, in_=s)
-            elif engine == "vector":
-                nc.vector.tensor_copy(out=d, in_=s)
-            else:
+            if engine == "gpsimd":
                 nc.gpsimd.tensor_scalar(out=dst, in0=src.rearrange("p j w -> p w j"), scalar1=1.0, scalar2=0.0,
                                         op0=ALU.mult, op1=ALU.add)
+                return
+            dst_walk = dst.rearrange("p (c i) j -> p c j i", i=4)
+            src_walk = src.rearrange("p j (c i) -> p c j i", i=4)
+            if engine == "scalar":
+                nc.scalar.copy(out=dst_walk, in_=src_walk)
+            else:
+                nc.vector.tensor_copy(out=dst_walk, in_=src_walk)
 
         def group_operand(k, engine, lo, hi):
             if ("grouped", k) not in tiles:
@@ -144,31 +161,37 @@ def tile_lstm_cell_pa_v_kernel(
             if hi > lo:
                 interleave(engine, tiles["grouped", k][:, lo:hi, :], tiles["raw", k][:, :, lo:hi])
 
-        op_codes = sb.tile([P, 8, I], U32, name="op_codes", align_bytes=64)
-        op_scales = sb.tile([P, 8, I], U8, name="op_scales", align_bytes=64)
+        def operand_shares(n):
+            shares = []
+            for place, k in enumerate(operands_at(n, 1, PARK_PERIOD)):
+                pool_end = POOL_COLS if n >= 1 and place == 0 else 0
+                vector_end = I if n in DW_PERIODS else I // 2 if n == PARK_PERIOD else pool_end
+                shares.append((k, pool_end, vector_end))
+            return shares
+
+        op_codes = sb.tile([P, OPERANDS, I], U32, name="op_codes", align_bytes=64)
+        op_scales = sb.tile([P, OPERANDS, I], U8, name="op_scales", align_bytes=64)
 
         def quantise_operand(k):
-            nc.vector.quantize_mx(
-                out=op_codes[:, k, :].bitcast(E4M3), scales=op_scales[:, k, :],
-                in_=tiles["grouped", k][:].rearrange("p w j -> p (w j)"),
-            )
+            nc.vector.quantize_mx(out=op_codes[:, k, :].bitcast(E4M3), scales=op_scales[:, k, :],
+                                  in_=tiles["grouped", k][:].rearrange("p w j -> p (w j)"))
 
         ident = sb.tile([P, P], F32, name="ident", align_bytes=64)
         ident_bf = sb.tile([P, P], BF16, name="ident_bf", align_bytes=64)
         last_rows = sb.tile([P, 2, K_PASS], BF16, name="last_rows", align_bytes=64)
 
         def turn_last_step(q):
-            bk = bank("tr", [P, 2, 4, P], BF16)
+            bk = bank("ct", [P, 2, 2 * FT, P], BF16)
             for k in range(2):
-                for ft in range(4):
+                for ft in range(2 * FT):
                     nc.tensor.transpose(bk[:, k, ft, :], last_rows[:, k, ft * P:(ft + 1) * P], ident_bf[:])
-            g1_t = ring("g1_t", 2, [P, 4, P], BF16)
-            g2_neg_t = ring("g2_neg_t", 2, [P, 4, P], F32)
-            nc.scalar.copy(out=g1_t[:], in_=bk[:, 0, :, :])
-            nc.scalar.activation(out=g2_neg_t[:], in_=bk[:, 1, :, :], func=ACT.Copy, scale=-1.0)
-            tiles["g1_t", q], tiles["g2_neg_t", q] = g1_t, g2_neg_t
+            g1_turned = ring("g1_turned", 2, [P, 2 * FT, P], BF16)
+            g2_neg_turned = ring("g2_neg_turned", 2, [P, 2 * FT, P], F32)
+            nc.scalar.copy(out=g1_turned[:], in_=bk[:, 0, :, :])
+            nc.scalar.activation(out=g2_neg_turned[:], in_=bk[:, 1, :, :], func=ACT.Copy, scale=-1.0)
+            tiles["g1", q], tiles["g2", q] = g1_turned, g2_neg_turned
 
-        def prod_a(n, engine, lo=0, hi=CW):
+        def product_a(n, engine, lo=0, hi=CW):
             if n >= CHUNKS:
                 return
             if lo == 0:
@@ -177,7 +200,7 @@ def tile_lstm_cell_pa_v_kernel(
             c0_b = tiles["c0", n // 2][:, c_lo + lo:c_lo + hi].unsqueeze(1).to_broadcast([P, PACK, hi - lo])
             engine.tensor_tensor(out=tiles["a", n][:, :, lo:hi], in0=tiles["f", n][:, :, lo:hi], in1=c0_b, op=ALU.mult)
 
-        def prod_b(n, lo=0, hi=CW):
+        def product_b(n, lo=0, hi=CW):
             if lo == 0:
                 tiles["b", n] = ring("b", 2, [P, PACK, CW], F32)
             nc.vector.tensor_tensor(out=tiles["b", n][:, :, lo:hi], in0=tiles["i", n][:, :, lo:hi],
@@ -185,197 +208,201 @@ def tile_lstm_cell_pa_v_kernel(
 
         def square_g(n):
             g = tiles["g", n]
-            if n == CHUNKS - 1:
-                sg = ring("a", 2, [P, PACK, CW], F32)
-                nc.gpsimd.tensor_tensor(out=sg[:], in0=g[:], in1=g[:], op=ALU.mult)
+            if n == LAST:
+                g_sq = ring("a", 2, [P, PACK, CW], F32)
+                nc.gpsimd.tensor_tensor(out=g_sq[:], in0=g[:], in1=g[:], op=ALU.mult)
             else:
-                sg = ring("sg", 2, [P, PACK, CW], F32)
-                nc.scalar.activation(out=sg[:], in_=g[:], func=ACT.Square)
-            tiles["sg", n] = sg
+                g_sq = ring("g_sq", 2, [P, PACK, CW], F32)
+                nc.scalar.activation(out=g_sq[:], in_=g[:], func=ACT.Square)
+            tiles["g_sq", n] = g_sq
 
         def add_transposed(out, terms):
             for k, term in enumerate(terms):
                 nc.tensor.matmul(out, lhsT=term, rhs=ident[:], is_transpose=True,
                                  start=(k == 0), stop=(k == len(terms) - 1))
 
-        def cell_state(n, fts=(0, 1)):
+        def cell_state(n, fts=range(FT)):
             for ft in fts:
                 bk = bank("ct", [P, PACK, P], F32)
+                cols = slice(ft * P, (ft + 1) * P)
                 for j in range(PACK):
-                    cols = slice(ft * P, (ft + 1) * P)
                     add_transposed(bk[:, j, :], [tiles["a", n][:, j, cols], tiles["b", n][:, j, cols]])
-                tiles["ct", n, ft] = bk
+                tiles["c", n, ft] = bk
 
-        def tanh_c(n, fts=(0, 1)):
+        def tanh_c(n, fts=range(FT)):
             for ft in fts:
                 if ft == 0:
-                    tiles["hs", n] = ring("hs", 1, [P, 2, PACK, P], F32)
-                nc.scalar.activation(out=tiles["hs", n][:, ft, :, :], in_=tiles["ct", n, ft][:], func=ACT.Tanh)
+                    tiles["h", n] = ring("h", 1, [P, FT, PACK, P], F32)
+                nc.scalar.activation(out=tiles["h", n][:, ft, :, :], in_=tiles["c", n, ft][:], func=ACT.Tanh)
 
-        def square_h(n, lo=0, hi=2):
-            hs = tiles["hs", n][:, lo:hi, :, :]
-            nc.scalar.activation(out=hs, in_=hs, func=ACT.Square)
+        def square_h(n, lo=0, hi=FT):
+            h = tiles["h", n][:, lo:hi, :, :]
+            nc.scalar.activation(out=h, in_=h, func=ACT.Square)
 
         def minus_one_times(out, in0, in1):
             nc.vector.scalar_tensor_tensor(out=out, in0=in0, scalar=1.0, in1=in1, op0=ALU.subtract, op1=ALU.mult)
 
-        def dc_turned(n):
-            hs, gr = tiles["hs", n], tiles["grad", n]
-            dct = ring("dct", 1, [P, 2, PACK, P], F32)
-            extra = ring("extra", 1, [P, 2, P], F32)
-            for ft in range(2):
+        def dc_feature_major(n):
+            h_sq, grad = tiles["h", n], tiles["grad", n]
+            dc_turned = ring("dc_turned", 1, [P, FT, PACK, P], F32)
+            dc_last = ring("dc_last", 1, [P, FT, P], F32)
+            for ft in range(FT):
                 minus_one_times(
-                    dct[:, ft, :, :].rearrange("p j (b th) -> p (j b) th", th=2),
-                    hs[:, ft, :, :].rearrange("p j (b th) -> p (j b) th", th=2),
-                    gr[:, ft, :, :].rearrange("p (th j) b -> p (j b) th", th=2),
+                    dc_turned[:, ft, :, :].rearrange("p j (b th) -> p (j b) th", th=2),
+                    h_sq[:, ft, :, :].rearrange("p j (b th) -> p (j b) th", th=2),
+                    grad[:, ft, :, :].rearrange("p (th j) b -> p (j b) th", th=2),
                 )
-            ft0 = 2 * (n % 2)
-            minus_one_times(extra[:], hs[:, :, PACK - 1, :], tiles["g1_t", n // 2][:, ft0:ft0 + 2, :])
-            tiles["dct", n], tiles["extra", n] = dct, extra
+            ft0 = FT * (n % 2)
+            minus_one_times(dc_last[:], h_sq[:, :, PACK - 1, :], tiles["g1", n // 2][:, ft0:ft0 + FT, :])
+            tiles["dc_turned", n], tiles["dc_last", n] = dc_turned, dc_last
 
-        def dc_back(n):
-            dct, extra = tiles["dct", n], tiles["extra", n]
-            ft0 = 2 * (n % 2)
-            banks = []
+        def dc_token_major(n):
+            ft0 = FT * (n % 2)
             for jp in range(2):
                 bk = bank("dc", [P, 2, CW], F32)
                 for jj in range(2):
                     j = 2 * jp + jj
-                    for ft in range(2):
-                        terms = [dct[:, ft, j, :]]
+                    for ft in range(FT):
+                        terms = [tiles["dc_turned", n][:, ft, j, :]]
                         if j == PACK - 1:
-                            terms = terms + [extra[:, ft, :], tiles["g2_neg_t", n // 2][:, ft0 + ft, :]]
+                            terms.extend([tiles["dc_last", n][:, ft, :], tiles["g2", n // 2][:, ft0 + ft, :]])
                         add_transposed(bk[:, jj, ft * P:(ft + 1) * P], terms)
-                banks.append(bk)
-            tiles["dc", n] = banks
+                tiles["dc", n, jp] = bk
 
         def factor_i(n):
             b = tiles["b", n]
             minus_one_times(b[:], tiles["i", n][:], b[:])
-            tiles["u", GATE_I, n] = b
+            tiles["factor", GATE_I, n] = b
 
         def factor_g(n):
-            sg = tiles["sg", n]
-            minus_one_times(sg[:], sg[:], tiles["i", n][:])
-            tiles["u", GATE_G, n] = sg
+            g_sq = tiles["g_sq", n]
+            minus_one_times(g_sq[:], g_sq[:], tiles["i", n][:])
+            tiles["factor", GATE_G, n] = g_sq
 
         def factor_f(n):
             f = tiles["f", n]
             minus_one_times(f[:], f[:], tiles["a", n][:])
-            tiles["u", GATE_F, n] = f
+            tiles["factor", GATE_F, n] = f
 
-        def dz_view(n, gate):
+        def dz_piece(n, gate):
             s, side = divmod(3 * (n % 2) + GATE_ORDER.index(gate), 2)
             if ("dz", n // 2, s) not in tiles:
                 tiles["dz", n // 2, s] = ring("dz", 6, [P, PACK, K_PASS], BF16)
             return tiles["dz", n // 2, s][:, :, side * CW:(side + 1) * CW]
 
         def round_dz(n, gate):
-            dz = dz_view(n, gate)
+            dz = dz_piece(n, gate)
             for jp in range(2):
                 js = slice(2 * jp, 2 * jp + 2)
-                nc.vector.tensor_tensor(out=dz[:, js, :], in0=tiles["dc", n][jp][:],
-                                        in1=tiles["u", gate, n][:, js, :], op=ALU.mult)
+                nc.vector.tensor_tensor(out=dz[:, js, :], in0=tiles["dc", n, jp][:],
+                                        in1=tiles["factor", gate, n][:, js, :], op=ALU.mult)
 
         def group_tokens(n, gate, engine):
-            if ("tokg", n) not in tiles:
-                tiles["tokg", n] = ring("tokg", 2, [P, 3, CW, PACK], BF16)
-            interleave(engine, tiles["tokg", n][:, GATE_ORDER.index(gate), :, :], dz_view(n, gate))
+            if ("token_grouped", n) not in tiles:
+                tiles["token_grouped", n] = ring("token_grouped", 2, [P, 3, CW, PACK], BF16)
+            interleave(engine, tiles["token_grouped", n][:, GATE_ORDER.index(gate), :, :], dz_piece(n, gate))
 
         def quantise_tokens(n, lo, hi):
-            if ("tok", n) not in tiles:
-                tiles["tok", n] = (ring("tokc", 4, [P, 3, CW], U32), ring("toks", 4, [P, 3, CW], U8))
-            codes, scales = tiles["tok", n]
+            if ("token_q", n) not in tiles:
+                tiles["token_q", n] = (ring("token_codes", 4, [P, 3, CW], U32), ring("token_scales", 4, [P, 3, CW], U8))
+            codes, scales = tiles["token_q", n]
             nc.vector.quantize_mx(out=codes[:, lo:hi, :].rearrange("p k w -> p (k w)").bitcast(E5M2),
                                   scales=scales[:, lo:hi, :].rearrange("p k w -> p (k w)"),
-                                  in_=tiles["tokg", n][:, lo:hi, :, :].rearrange("p k w j -> p (k w j)"))
+                                  in_=tiles["token_grouped", n][:, lo:hi, :, :].rearrange("p k w j -> p (k w j)"))
 
-        def drain(bk, dst, engine):
+        def quantise_all_gates(n):
+            quantise_tokens(n, 0, 2)
+            quantise_tokens(n, 2, 3)
+
+        def drain(bk, dst):
             stage = ring("stage", 8, [P, I], F32)
-            if engine == "scalar":
-                nc.scalar.copy(out=stage[:], in_=bk[:])
-            else:
-                nc.vector.tensor_copy(out=stage[:], in_=bk[:])
+            nc.scalar.copy(out=stage[:], in_=bk[:])
             nc.sync.dma_start(out=dst, in_=stage[:])
 
-        def dw_tile(n, gate, m, engine, kind="mx"):
-            bk = bank(kind, [P, I], F32)
+        def weight_gradient(n, gate, kind):
             place = GATE_ORDER.index(gate)
-            for g in range(2):
-                codes, scales = tiles["tok", n - 2 + 2 * g]
-                cols = slice(m * P, (m + 1) * P)
-                nc.tensor.matmul_mx(out=bk[:], lhsT=codes[:, place, cols].bitcast(E5M2), lhsT_scale=scales[:, place, cols],
-                                    rhs=op_codes[:, g, :].bitcast(E4M3), rhs_scale=op_scales[:, g, :],
-                                    start=(g == 0), stop=(g == 1))
-            r0 = col0(n) + m * P
-            drain(bk, dw_out[gate][r0:r0 + P, :], engine)
+            for ft in range(FT):
+                bk = bank(kind, [P, I], F32)
+                cols = slice(ft * P, (ft + 1) * P)
+                for g in range(2):
+                    codes, scales = tiles["token_q", n - 2 + 2 * g]
+                    nc.tensor.matmul_mx(out=bk[:], lhsT=codes[:, place, cols].bitcast(E5M2), lhsT_scale=scales[:, place, cols],
+                                        rhs=op_codes[:, g, :].bitcast(E4M3), rhs_scale=op_scales[:, g, :],
+                                        start=(g == 0), stop=(g == 1))
+                f0 = first_feature(n) + ft * P
+                drain(bk, dw_out[gate][f0:f0 + P, :])
+
+        def transpose_dz(q, s, kind):
+            words = tiles["dz", q, s][:].rearrange("p j f -> p (j f)").bitcast(F32)
+            per_j = K_PASS // 2
+            for jp in range(2):
+                bk = bank(kind, [P, 2, 2, P], F32)
+                for jj in range(2):
+                    w0 = (2 * jp + jj) * per_j
+                    for u in range(2):
+                        nc.tensor.transpose(bk[:, jj, u, :], words[:, w0 + u:w0 + per_j:2], ident[:])
+                tiles["dz_turned", q, s, jp] = bk
+
+        def group_features(q, s):
+            grouped = ring("feature_grouped", 3, [P, K_PASS * PACK], BF16)
+            grouped_words = grouped[:].bitcast(F32).rearrange("q (j p u) -> q j p u", j=PACK, u=2)
+            for jp in range(2):
+                nc.scalar.copy(out=grouped_words[:, 2 * jp:2 * jp + 2, :, :],
+                               in_=tiles["dz_turned", q, s, jp][:].rearrange("q j u p -> q j p u"))
+            tiles["feature_grouped", q, s] = grouped
 
         def turn_dz(q, s):
-            words = tiles["dz", q, s][:].rearrange("p j f -> p (j f)").bitcast(F32)
-            t = ring("grp", 3, [P, PACK * P * PACK], BF16)
-            t_words = t[:].bitcast(F32).rearrange("q (j p u) -> q j p u", j=PACK, u=2)
-            for jp in range(2):
-                bk = bank("tr", [P, 2, 2, P], F32)
-                for jj in range(2):
-                    w0 = (2 * jp + jj) * 256
-                    for u in range(2):
-                        nc.tensor.transpose(bk[:, jj, u, :], words[:, w0 + u:w0 + 256:2], ident[:])
-                nc.scalar.copy(out=t_words[:, 2 * jp:2 * jp + 2, :, :], in_=bk[:].rearrange("q j u p -> q j p u"))
-            tiles["featg", q, s] = t
+            transpose_dz(q, s, "tr")
+            group_features(q, s)
 
         def quantise_features(q, s):
-            codes = ring("featc", 9, [P, K_PASS], U32)
-            scales = ring("feats", 9, [P, K_PASS], U8)
-            nc.vector.quantize_mx(out=codes[:].bitcast(E5M2), scales=scales[:], in_=tiles["featg", q, s][:])
-            tiles["feat", q, s] = (codes, scales)
+            codes = ring("feature_codes", 9, [P, K_PASS], U32)
+            scales = ring("feature_scales", 9, [P, K_PASS], U8)
+            nc.vector.quantize_mx(out=codes[:].bitcast(E5M2), scales=scales[:], in_=tiles["feature_grouped", q, s][:])
+            tiles["feature_q", q, s] = (codes, scales)
 
-        def dx_passes(key, g, j, passes, kind, opens, closes):
-            if opens:
-                tiles["dx", key, j] = bank(kind, [P, I], F32)
-            bk = tiles["dx", key, j]
-            for idx, k in enumerate(passes):
-                h, s = divmod(k, 3)
-                codes, scales = tiles["feat", 2 * h + g, s]
-                cols = slice(j * P, (j + 1) * P)
-                nc.tensor.matmul_mx(out=bk[:], lhsT=codes[:, cols].bitcast(E5M2), lhsT_scale=scales[:, cols],
+        def dx_passes(g, j, passes, open_in, closes):
+            if open_in:
+                tiles["dx", g, j] = bank(open_in, [P, I], F32)
+            cols = slice(j * P, (j + 1) * P)
+            for k in passes:
+                half, s = divmod(k, 3)
+                codes, scales = tiles["feature_q", 2 * half + g, s]
+                nc.tensor.matmul_mx(out=tiles["dx", g, j][:], lhsT=codes[:, cols].bitcast(E5M2), lhsT_scale=scales[:, cols],
                                     rhs=op_codes[:, 2 + k, :].bitcast(E4M3), rhs_scale=op_scales[:, 2 + k, :],
-                                    start=(opens and idx == 0), stop=(closes and idx == len(passes) - 1))
+                                    start=(bool(open_in) and k == passes[0]), stop=(closes and k == passes[-1]))
 
-        def dx_drain(j):
-            drain(tiles["dx", "g0", j], dx_rows[0, :, j, :], "scalar")
-
-        dx_part = sb.tile([P, PACK, I], F32, name="dx_part", align_bytes=64)
+        dx_parked = sb.tile([P, PACK, I], F32, name="dx_parked", align_bytes=64)
 
         def dx_park(j):
-            dx_passes("park", 1, j, (0, 1, 2), "mx", True, True)
-            nc.scalar.copy(out=dx_part[:, j, :], in_=tiles["dx", "park", j][:])
+            dx_passes(1, j, (0, 1, 2), "mx", True)
+            nc.scalar.copy(out=dx_parked[:, j, :], in_=tiles["dx", 1, j][:])
 
         def dx_finish(j):
-            nc.vector.tensor_tensor(out=dx_part[:, j, :], in0=tiles["dx", "g1", j][:], in1=dx_part[:, j, :], op=ALU.add)
-            nc.sync.dma_start(out=dx_rows[1, :, j, :], in_=dx_part[:, j, :])
+            nc.vector.tensor_tensor(out=dx_parked[:, j, :], in0=tiles["dx", 1, j][:], in1=dx_parked[:, j, :], op=ALU.add)
+            nc.sync.dma_start(out=dx_rows[1, :, j, :], in_=dx_parked[:, j, :])
 
-        first, second, third = GATE_ORDER
         load_ig(0, 0, P)
         load_f(0, 0, P)
-        load_quarter(0)
+        load_c0(0)
         load_ig(0, P, CW)
         load_f(0, P, CW)
         load_grad(0)
-        nc.vector.memset(last_rows[:].rearrange("p g w -> p (g w)").bitcast(U32), 0)
+        nc.vector.memset(last_rows[:].rearrange("p k w -> p (k w)").bitcast(U32), 0)
         make_identity(nc, ident[:])
         make_identity(nc, ident_bf[:])
         load_last_step(0)
         load_operand(0)
         load_f(1)
         load_ig(1)
-        load_quarter(1)
+        load_c0(1)
         load_f(2)
         load_grad(1)
         load_operand(1)
 
-        for ft in range(2):
-            prod_b(0, ft * P, (ft + 1) * P)
-            prod_a(0, nc.vector, ft * P, (ft + 1) * P)
+        for ft in range(FT):
+            product_b(0, ft * P, (ft + 1) * P)
+            product_a(0, nc.vector, ft * P, (ft + 1) * P)
             cell_state(0, (ft,))
             tanh_c(0, (ft,))
             square_h(0, ft, ft + 1)
@@ -387,129 +414,125 @@ def tile_lstm_cell_pa_v_kernel(
         load_ig(2)
         group_operand(0, "scalar", 0, I)
 
-        def dw_pair(n, gate):
-            for m in range(2):
-                dw_tile(n, gate, m, "scalar")
-
-        def ready_passes(n):
-            if n < 0:
-                return []
-            return [(n // 2, s) for s in ((0,) if n % 2 == 0 else (1, 2))]
-
-        for n in range(CHUNKS - 1):
-            turns = ready_passes(n - 1)
-            dc_turned(n)
+        for n in range(LAST):
+            turns = passes_completed_by(n - 1)
+            turns_first = turns if n == DX0_PERIOD else []
+            turns_later = [] if n == DX0_PERIOD else turns
+            dc_feature_major(n)
             if n > 0:
                 load_ig(n + 2)
-            if n % 2 == 0 and n < 6:
+            if n % 2 == 0 and n // 2 + 1 < QUARTERS:
                 load_last_step(n // 2 + 1)
             load_grad(n + 2)
             load_f(n + 3)
             if n % 2 == 1:
-                load_quarter(n // 2 + 2)
-            for k in OPERAND_LOADS.get(n, ()):
+                load_c0(n // 2 + 2)
+            for k in operands_at(n, 2, PARK_PERIOD - 1):
                 load_operand(k)
-            if n == 6:
-                turn_dz(*turns[0])
-            if n >= 1:
+            for q, s in turns_first[:1]:
+                turn_dz(q, s)
+            if n > 0:
                 group_tokens(n - 1, first, "scalar")
-            dc_back(n)
+            dc_token_major(n)
             if n == 0:
-                prod_a(1, nc.vector)
+                product_a(1, nc.vector)
                 factor_f(0)
-            prod_b(n + 1)
-            if n == 6:
-                turn_dz(*turns[1])
-            if n >= 1:
+            product_b(n + 1)
+            for q, s in turns_first[1:]:
+                turn_dz(q, s)
+            if n > 0:
                 group_tokens(n - 1, second, "scalar")
             cell_state(n + 1)
-            if n >= 1:
+            if n > 0:
                 group_tokens(n - 1, third, "scalar")
-            for q, s in ready_passes(n - 2):
+            for q, s in passes_completed_by(n - 2):
                 quantise_features(q, s)
-            if n >= 1:
+            if n > 0:
                 factor_i(n)
-                factor_g(n)
-            for k in OPERAND_QUANT.get(n, ()):
-                quantise_operand(k)
+            if n == 1:
+                quantise_operand(0)
+            if n > 0:
+                for k in operands_at(n, 0, DX0_PERIOD):
+                    quantise_operand(k)
             tanh_c(n + 1)
-            if n == 6:
-                for q, s in turns:
+            if n == DX0_PERIOD:
+                for q, s in turns_first:
                     quantise_features(q, s)
                 for j in (0, 1):
-                    dx_passes("g0", 0, j, (3, 4, 5), None, False, True)
+                    dx_passes(0, j, (3, 4, 5), None, True)
                 for j in (2, 3):
-                    dx_passes("g0", 0, j, range(6), "ct", True, True)
-            if n >= 1:
-                quantise_tokens(n - 1, 0, 2)
-                quantise_tokens(n - 1, 2, 3)
-            if n >= 1:
+                    dx_passes(0, j, range(6), "ct", True)
+            if n > 0 and token_pass(n - 1) == 1:
+                quantise_all_gates(n - 1)
+            if n > 0:
                 factor_f(n)
-            prod_a(n + 2, nc.gpsimd)
-            for k, to_pool, to_vector in OPERAND_GROUP.get(n, ()):
-                group_operand(k, "gpsimd", 0, to_pool)
+                factor_g(n)
+            product_a(n + 2, nc.gpsimd)
+            for k, pool_end, vector_end in operand_shares(n):
+                group_operand(k, "gpsimd", 0, pool_end)
             for gate in GATE_ORDER:
                 round_dz(n, gate)
-            steps = [lambda: square_h(n + 1), lambda: square_g(n + 1), lambda: None]
-            for place, step in enumerate(steps):
-                if n != 6 and place < len(turns):
-                    turn_dz(*turns[place])
-                step()
-                if n in (3, 4):
-                    dw_pair(n - 1, GATE_ORDER[place])
-                if n == 5 and place < 2:
-                    for j in (2 * place, 2 * place + 1):
+            if n > 0 and token_pass(n - 1) == 0:
+                quantise_all_gates(n - 1)
+            for place, gate in enumerate(GATE_ORDER):
+                for q, s in turns_later[place:place + 1]:
+                    turn_dz(q, s)
+                if place == 0:
+                    square_h(n + 1)
+                    if n % 2 == 1:
+                        turn_last_step(n // 2 + 1)
+                if place == 1:
+                    square_g(n + 1)
+                if n in DW_PERIODS:
+                    weight_gradient(n - 1, gate, "mx")
+                if n == PARK_PERIOD:
+                    for j in range(PACK)[2 * place:2 * place + 2]:
                         dx_park(j)
-            if n % 2 == 1 and n < 6:
-                turn_last_step(n // 2 + 1)
-            for k, to_pool, to_vector in OPERAND_GROUP.get(n, ()):
-                group_operand(k, "vector", to_pool, to_pool + to_vector)
-                group_operand(k, "scalar", to_pool + to_vector, I)
-            if n == 5:
+            for k, pool_end, vector_end in operand_shares(n):
+                group_operand(k, "vector", pool_end, vector_end)
+                group_operand(k, "scalar", vector_end, I)
+            if n == PARK_PERIOD:
                 for j in (0, 1):
-                    dx_passes("g0", 0, j, (0, 1, 2), "mx", True, False)
-            if n == 6:
+                    dx_passes(0, j, (0, 1, 2), "mx", False)
+            if n == DX0_PERIOD:
                 for j in range(PACK):
-                    dx_drain(j)
+                    drain(tiles["dx", 0, j], dx_rows[0, :, j, :])
 
-        n = CHUNKS - 1
-        dc_turned(n)
+        q = QUARTERS - 1
+        dc_feature_major(LAST)
         for gate in GATE_ORDER:
-            group_tokens(n - 1, gate, "scalar")
-        dc_back(n)
-        turn_dz(3, 0)
-        factor_i(n)
-        factor_g(n)
-        quantise_tokens(n - 1, 0, 2)
-        quantise_tokens(n - 1, 2, 3)
-        factor_f(n)
-        quantise_features(3, 0)
-        for place, gate in enumerate(GATE_ORDER):
-            for m in range(2):
-                dw_tile(n - 1, gate, m, "scalar", "ct" if place == 1 else "mx")
-        round_dz(n, first)
+            group_tokens(LAST - 1, gate, "scalar")
+        dc_token_major(LAST)
+        turn_dz(q, 0)
+        factor_i(LAST)
+        factor_g(LAST)
+        quantise_all_gates(LAST - 1)
+        factor_f(LAST)
+        quantise_features(q, 0)
+        for gate, kind in ((first, "mx"), (second, "ct"), (third, "mx")):
+            weight_gradient(LAST - 1, gate, kind)
+        round_dz(LAST, first)
+        transpose_dz(q, 1, "tr")
         for j in (0, 1):
-            dx_passes("g1", 1, j, (3,), "ct", True, False)
-        turn_dz(3, 1)
+            dx_passes(1, j, (3,), "ct", False)
+        round_dz(LAST, second)
+        round_dz(LAST, third)
+        transpose_dz(q, 2, "dc")
         for j in (2, 3):
-            dx_passes("g1", 1, j, (3,), "mx", True, False)
-        round_dz(n, second)
-        round_dz(n, third)
-        turn_dz(3, 2)
-        group_tokens(n, first, "vector")
-        quantise_features(3, 1)
-        quantise_tokens(n, 0, 1)
-        group_tokens(n, second, "vector")
-        group_tokens(n, third, "scalar")
-        quantise_features(3, 2)
-        quantise_tokens(n, 1, 2)
-        quantise_tokens(n, 2, 3)
-        dw_tile(n, first, 0, "scalar", "dc")
-        dw_tile(n, first, 1, "scalar", "dc")
+            dx_passes(1, j, (3,), "mx", False)
+        group_features(q, 1)
+        group_features(q, 2)
+        group_tokens(LAST, first, "vector")
+        group_tokens(LAST, second, "vector")
+        quantise_tokens(LAST, 0, 1)
+        group_tokens(LAST, third, "vector")
+        quantise_tokens(LAST, 1, 2)
+        quantise_features(q, 1)
+        quantise_features(q, 2)
+        quantise_tokens(LAST, 2, 3)
+        weight_gradient(LAST, first, "tr")
+        weight_gradient(LAST, second, "dc")
         for j in range(PACK):
-            dx_passes("g1", 1, j, (4, 5), None, False, True)
+            dx_passes(1, j, (4, 5), None, True)
             dx_finish(j)
-        dw_tile(n, second, 0, "scalar", "tr")
-        dw_tile(n, second, 1, "scalar", "tr")
-        dw_tile(n, third, 0, "scalar", "dc")
-        dw_tile(n, third, 1, "vector", "dc")
+        weight_gradient(LAST, third, "tr")

@@ -33,7 +33,7 @@ OPERANDS = 8
 DW_PERIODS = (3, 4)
 PARK_PERIOD = 5
 DX0_PERIOD = 6
-POOL_COLS = 128
+POOL_COLS = 192
 
 
 def tile_lstm_cell_pa_v_kernel(
@@ -404,13 +404,13 @@ def tile_lstm_cell_pa_v_kernel(
             product_b(0, ft * P, (ft + 1) * P)
             product_a(0, nc.vector, ft * P, (ft + 1) * P)
             cell_state(0, (ft,))
-            tanh_c(0, (ft,))
-            square_h(0, ft, ft + 1)
             if ft == 0:
                 square_g(0)
+            tanh_c(0, (ft,))
+            square_h(0, ft, ft + 1)
         turn_last_step(0)
-        factor_i(0)
         factor_g(0)
+        factor_i(0)
         load_ig(2)
         group_operand(0, "scalar", 0, I)
 
@@ -454,17 +454,24 @@ def tile_lstm_cell_pa_v_kernel(
             if n > 0:
                 for k in operands_at(n, 0, DX0_PERIOD):
                     quantise_operand(k)
-            tanh_c(n + 1)
+            if n == 0:
+                for ft in range(FT):
+                    tanh_c(1, (ft,))
+                    square_h(1, ft, ft + 1)
+            else:
+                tanh_c(n + 1)
+            if n > 0 and token_pass(n - 1) == 1:
+                quantise_all_gates(n - 1)
             if n == DX0_PERIOD:
-                for q, s in turns_first:
-                    quantise_features(q, s)
+                factor_g(n)
+                quantise_features(*turns_first[0])
+                factor_f(n)
+                quantise_features(*turns_first[1])
                 for j in (0, 1):
                     dx_passes(0, j, (3, 4, 5), None, True)
                 for j in (2, 3):
                     dx_passes(0, j, range(6), "ct", True)
-            if n > 0 and token_pass(n - 1) == 1:
-                quantise_all_gates(n - 1)
-            if n > 0:
+            elif n > 0:
                 factor_f(n)
                 factor_g(n)
             product_a(n + 2, nc.gpsimd)
@@ -477,7 +484,7 @@ def tile_lstm_cell_pa_v_kernel(
             for place, gate in enumerate(GATE_ORDER):
                 for q, s in turns_later[place:place + 1]:
                     turn_dz(q, s)
-                if place == 0:
+                if place == 0 and n > 0:
                     square_h(n + 1)
                     if n % 2 == 1:
                         turn_last_step(n // 2 + 1)

from contextlib import ExitStack

import concourse.mybir as mybir
from concourse.masks import make_identity

B, T, I, H = 128, 8, 512, 1024
TOKENS = B * T
FLOPS = 2 * 2 * TOKENS * 3 * H * I
BYTES = 3 * TOKENS * H * 4 + TOKENS * H * 2 + 3 * B * H * 2 + 3 * H * I * 2 + TOKENS * I * 2 + (TOKENS + 3 * H) * I * 4

F32 = mybir.dt.float32
BF16 = mybir.dt.bfloat16
U32 = mybir.dt.uint32
U8 = mybir.dt.uint8
E4M3 = mybir.dt.float8_e4m3fn_x4
E5M2 = mybir.dt.float8_e5m2_x4
ALU = mybir.AluOpType
ACT = mybir.ActivationFunctionType

P = 128
PACK = 4
K_PASS = P * PACK
CW = 256
FT = CW // P
ROWS = B // 2
CHUNKS = 8
QUARTERS = CHUNKS // 2
LAST = CHUNKS - 1
GATE_F, GATE_I, GATE_G = 0, 1, 2
GATE_ORDER = (GATE_I, GATE_F, GATE_G)
OPERANDS = 8

DW_PERIODS = (3, 4)
PARK_PERIOD = 5
DX0_PERIOD = 6
POOL_COLS = 192


def tile_lstm_cell_pa_v_kernel(
    tc, x, h0, c0, W_f, b_f, R_f, rb_f, W_i, b_i, R_i, rb_i, W_g, b_g, R_g, rb_g,
    f_t, i_t, g_t, grad_0, grad_1, grad_2, out_0, out_1, out_2, out_3,
):
    nc = tc.nc
    weights = (W_f, W_i, W_g)
    dw_out = (out_1, out_2, out_3)
    first, second, third = GATE_ORDER

    def by_token_pass(ap):
        return ap.rearrange("b t w -> (b t) w").rearrange("(g p j) w -> g p j w", g=2, j=PACK)

    saved = {"f": by_token_pass(f_t), "i": by_token_pass(i_t), "g": by_token_pass(g_t)}
    x_rows = by_token_pass(x)
    dx_rows = by_token_pass(out_0)
    grad_cols = grad_0.rearrange("f (t g b) -> f t g b", t=T, g=2)

    def token_pass(n):
        return (n // 2) % 2

    def first_feature(n):
        return (n // 4) * K_PASS + (n % 2) * CW

    def passes_completed_by(n):
        if n < 0:
            return []
        return [(n // 2, s) for s in ((0,) if n % 2 == 0 else (1, 2))]

    def operands_at(n, lead, latest):
        return [k for k in range(OPERANDS) if min(k - lead, latest) == n]

    with ExitStack() as ctx:
        sb = ctx.enter_context(tc.tile_pool(name="sb", bufs=1))
        ps = ctx.enter_context(tc.psum_pool(name="ps", bufs=1))
        ctx.enter_context(tc.manual_schedule())

        tiles = {}
        handed_out = {}

        def next_tag(kind, slots):
            count = handed_out.get(kind, 0)
            handed_out[kind] = count + 1
            return "%s%d" % (kind, count % slots)

        def ring(kind, slots, shape, dtype):
            tag = next_tag(kind, slots)
            return sb.tile(shape, dtype, name=tag, tag=tag, align_bytes=64)

        def bank(kind, shape, dtype):
            tag = next_tag(kind, 2)
            return ps.tile(shape, dtype, name=tag, tag=tag)

        def load_saved(kind, slots, n, lo, hi):
            if n >= CHUNKS:
                return
            if lo == 0:
                tiles[kind, n] = ring("in_" + kind, slots, [P, PACK, CW], F32)
            f0 = first_feature(n)
            nc.sync.dma_start(out=tiles[kind, n][:, :, lo:hi], in_=saved[kind][token_pass(n), :, :, f0 + lo:f0 + hi])

        def load_f(n, lo=0, hi=CW):
            load_saved("f", 4, n, lo, hi)

        def load_ig(n, lo=0, hi=CW):
            load_saved("i", 3, n, lo, hi)
            load_saved("g", 2, n, lo, hi)

        def load_grad(n):
            if n >= CHUNKS:
                return
            grad = ring("grad", 3, [P, FT, T, ROWS], BF16)
            for ft in range(FT):
                f0 = first_feature(n) + ft * P
                nc.sync.dma_start(out=grad[:, ft, :, :], in_=grad_cols[f0:f0 + P, :, token_pass(n), :])
            tiles["grad", n] = grad

        def quarter_slices(q):
            half, g = divmod(q, 2)
            return slice(ROWS * g, ROWS * (g + 1)), slice(half * K_PASS, (half + 1) * K_PASS)

        def load_c0(q):
            if q >= QUARTERS:
                return
            rows, cols = quarter_slices(q)
            c0_rows = ring("c0_", 2, [P, K_PASS], BF16)
            for th in range(2):
                nc.sync.dma_start(out=c0_rows[th:P:2, :], in_=c0[rows, cols])
            tiles["c0", q] = c0_rows

        def load_last_step(q):
            rows, cols = quarter_slices(q)
            for k, src in enumerate((grad_1, grad_2)):
                nc.sync.dma_start(out=last_rows[1:P:2, k, :], in_=src[rows, cols])

        def load_operand(k):
            raw = ring("raw", 3, [P, PACK, I], BF16)
            if k < 2:
                nc.sync.dma_start(out=raw[:], in_=x_rows[k])
            else:
                half, s = divmod(k - 2, 3)
                for side in range(2):
                    chunk, place = divmod(2 * s + side, 3)
                    r0 = half * K_PASS + chunk * CW
                    src = weights[GATE_ORDER[place]][r0:r0 + CW, :].rearrange("(q r) w -> q r w", r=PACK)
                    nc.sync.dma_start(out=raw[side * P // 2:(side + 1) * P // 2, :, :], in_=src)
            tiles["raw", k] = raw

        def interleave(engine, dst, src):
            if engine == "gpsimd":
                nc.gpsimd.tensor_scalar(out=dst, in0=src.rearrange("p j w -> p w j"), scalar1=1.0, scalar2=0.0,
                                        op0=ALU.mult, op1=ALU.add)
                return
            dst_walk = dst.rearrange("p (c i) j -> p c j i", i=4)
            src_walk = src.rearrange("p j (c i) -> p c j i", i=4)
            if engine == "scalar":
                nc.scalar.copy(out=dst_walk, in_=src_walk)
            else:
                nc.vector.tensor_copy(out=dst_walk, in_=src_walk)

        def group_operand(k, engine, lo, hi):
            if ("grouped", k) not in tiles:
                tiles["grouped", k] = ring("opg", 2, [P, I, PACK], BF16)
            if hi > lo:
                interleave(engine, tiles["grouped", k][:, lo:hi, :], tiles["raw", k][:, :, lo:hi])

        def operand_shares(n):
            shares = []
            for place, k in enumerate(operands_at(n, 1, PARK_PERIOD)):
                pool_end = POOL_COLS if n >= 1 and place == 0 else 0
                vector_end = I if n in DW_PERIODS else I // 2 if n == PARK_PERIOD else pool_end
                shares.append((k, pool_end, vector_end))
            return shares

        op_codes = sb.tile([P, OPERANDS, I], U32, name="op_codes", align_bytes=64)
        op_scales = sb.tile([P, OPERANDS, I], U8, name="op_scales", align_bytes=64)

        def quantise_operand(k):
            nc.vector.quantize_mx(out=op_codes[:, k, :].bitcast(E4M3), scales=op_scales[:, k, :],
                                  in_=tiles["grouped", k][:].rearrange("p w j -> p (w j)"))

        ident = sb.tile([P, P], F32, name="ident", align_bytes=64)
        ident_bf = sb.tile([P, P], BF16, name="ident_bf", align_bytes=64)
        last_rows = sb.tile([P, 2, K_PASS], BF16, name="last_rows", align_bytes=64)

        def turn_last_step(q):
            bk = bank("ct", [P, 2, 2 * FT, P], BF16)
            for k in range(2):
                for ft in range(2 * FT):
                    nc.tensor.transpose(bk[:, k, ft, :], last_rows[:, k, ft * P:(ft + 1) * P], ident_bf[:])
            g1_turned = ring("g1_turned", 2, [P, 2 * FT, P], BF16)
            g2_neg_turned = ring("g2_neg_turned", 2, [P, 2 * FT, P], F32)
            nc.scalar.copy(out=g1_turned[:], in_=bk[:, 0, :, :])
            nc.scalar.activation(out=g2_neg_turned[:], in_=bk[:, 1, :, :], func=ACT.Copy, scale=-1.0)
            tiles["g1", q], tiles["g2", q] = g1_turned, g2_neg_turned

        def product_a(n, engine, lo=0, hi=CW):
            if n >= CHUNKS:
                return
            if lo == 0:
                tiles["a", n] = ring("a", 2, [P, PACK, CW], F32)
            c_lo = (n % 2) * CW
            c0_b = tiles["c0", n // 2][:, c_lo + lo:c_lo + hi].unsqueeze(1).to_broadcast([P, PACK, hi - lo])
            engine.tensor_tensor(out=tiles["a", n][:, :, lo:hi], in0=tiles["f", n][:, :, lo:hi], in1=c0_b, op=ALU.mult)

        def product_b(n, lo=0, hi=CW):
            if lo == 0:
                tiles["b", n] = ring("b", 2, [P, PACK, CW], F32)
            nc.vector.tensor_tensor(out=tiles["b", n][:, :, lo:hi], in0=tiles["i", n][:, :, lo:hi],
                                    in1=tiles["g", n][:, :, lo:hi], op=ALU.mult)

        def square_g(n):
            g = tiles["g", n]
            if n == LAST:
                g_sq = ring("a", 2, [P, PACK, CW], F32)
                nc.gpsimd.tensor_tensor(out=g_sq[:], in0=g[:], in1=g[:], op=ALU.mult)
            else:
                g_sq = ring("g_sq", 2, [P, PACK, CW], F32)
                nc.scalar.activation(out=g_sq[:], in_=g[:], func=ACT.Square)
            tiles["g_sq", n] = g_sq

        def add_transposed(out, terms):
            for k, term in enumerate(terms):
                nc.tensor.matmul(out, lhsT=term, rhs=ident[:], is_transpose=True,
                                 start=(k == 0), stop=(k == len(terms) - 1))

        def cell_state(n, fts=range(FT)):
            for ft in fts:
                bk = bank("ct", [P, PACK, P], F32)
                cols = slice(ft * P, (ft + 1) * P)
                for j in range(PACK):
                    add_transposed(bk[:, j, :], [tiles["a", n][:, j, cols], tiles["b", n][:, j, cols]])
                tiles["c", n, ft] = bk

        def tanh_c(n, fts=range(FT)):
            for ft in fts:
                if ft == 0:
                    tiles["h", n] = ring("h", 1, [P, FT, PACK, P], F32)
                nc.scalar.activation(out=tiles["h", n][:, ft, :, :], in_=tiles["c", n, ft][:], func=ACT.Tanh)

        def square_h(n, lo=0, hi=FT):
            h = tiles["h", n][:, lo:hi, :, :]
            nc.scalar.activation(out=h, in_=h, func=ACT.Square)

        def minus_one_times(out, in0, in1):
            nc.vector.scalar_tensor_tensor(out=out, in0=in0, scalar=1.0, in1=in1, op0=ALU.subtract, op1=ALU.mult)

        def dc_feature_major(n):
            h_sq, grad = tiles["h", n], tiles["grad", n]
            dc_turned = ring("dc_turned", 1, [P, FT, PACK, P], F32)
            dc_last = ring("dc_last", 1, [P, FT, P], F32)
            for ft in range(FT):
                minus_one_times(
                    dc_turned[:, ft, :, :].rearrange("p j (b th) -> p (j b) th", th=2),
                    h_sq[:, ft, :, :].rearrange("p j (b th) -> p (j b) th", th=2),
                    grad[:, ft, :, :].rearrange("p (th j) b -> p (j b) th", th=2),
                )
            ft0 = FT * (n % 2)
            minus_one_times(dc_last[:], h_sq[:, :, PACK - 1, :], tiles["g1", n // 2][:, ft0:ft0 + FT, :])
            tiles["dc_turned", n], tiles["dc_last", n] = dc_turned, dc_last

        def dc_token_major(n):
            ft0 = FT * (n % 2)
            for jp in range(2):
                bk = bank("dc", [P, 2, CW], F32)
                for jj in range(2):
                    j = 2 * jp + jj
                    for ft in range(FT):
                        terms = [tiles["dc_turned", n][:, ft, j, :]]
                        if j == PACK - 1:
                            terms.extend([tiles["dc_last", n][:, ft, :], tiles["g2", n // 2][:, ft0 + ft, :]])
                        add_transposed(bk[:, jj, ft * P:(ft + 1) * P], terms)
                tiles["dc", n, jp] = bk

        def factor_i(n):
            b = tiles["b", n]
            minus_one_times(b[:], tiles["i", n][:], b[:])
            tiles["factor", GATE_I, n] = b

        def factor_g(n):
            g_sq = tiles["g_sq", n]
            minus_one_times(g_sq[:], g_sq[:], tiles["i", n][:])
            tiles["factor", GATE_G, n] = g_sq

        def factor_f(n):
            f = tiles["f", n]
            minus_one_times(f[:], f[:], tiles["a", n][:])
            tiles["factor", GATE_F, n] = f

        def dz_piece(n, gate):
            s, side = divmod(3 * (n % 2) + GATE_ORDER.index(gate), 2)
            if ("dz", n // 2, s) not in tiles:
                tiles["dz", n // 2, s] = ring("dz", 6, [P, PACK, K_PASS], BF16)
            return tiles["dz", n // 2, s][:, :, side * CW:(side + 1) * CW]

        def round_dz(n, gate):
            dz = dz_piece(n, gate)
            for jp in range(2):
                js = slice(2 * jp, 2 * jp + 2)
                nc.vector.tensor_tensor(out=dz[:, js, :], in0=tiles["dc", n, jp][:],
                                        in1=tiles["factor", gate, n][:, js, :], op=ALU.mult)

        def group_tokens(n, gate, engine):
            if ("token_grouped", n) not in tiles:
                tiles["token_grouped", n] = ring("token_grouped", 2, [P, 3, CW, PACK], BF16)
            interleave(engine, tiles["token_grouped", n][:, GATE_ORDER.index(gate), :, :], dz_piece(n, gate))

        def quantise_tokens(n, lo, hi):
            if ("token_q", n) not in tiles:
                tiles["token_q", n] = (ring("token_codes", 4, [P, 3, CW], U32), ring("token_scales", 4, [P, 3, CW], U8))
            codes, scales = tiles["token_q", n]
            nc.vector.quantize_mx(out=codes[:, lo:hi, :].rearrange("p k w -> p (k w)").bitcast(E5M2),
                                  scales=scales[:, lo:hi, :].rearrange("p k w -> p (k w)"),
                                  in_=tiles["token_grouped", n][:, lo:hi, :, :].rearrange("p k w j -> p (k w j)"))

        def quantise_all_gates(n):
            quantise_tokens(n, 0, 2)
            quantise_tokens(n, 2, 3)

        def drain(bk, dst):
            stage = ring("stage", 8, [P, I], F32)
            nc.scalar.copy(out=stage[:], in_=bk[:])
            nc.sync.dma_start(out=dst, in_=stage[:])

        def weight_gradient(n, gate, kind):
            place = GATE_ORDER.index(gate)
            for ft in range(FT):
                bk = bank(kind, [P, I], F32)
                cols = slice(ft * P, (ft + 1) * P)
                for g in range(2):
                    codes, scales = tiles["token_q", n - 2 + 2 * g]
                    nc.tensor.matmul_mx(out=bk[:], lhsT=codes[:, place, cols].bitcast(E5M2), lhsT_scale=scales[:, place, cols],
                                        rhs=op_codes[:, g, :].bitcast(E4M3), rhs_scale=op_scales[:, g, :],
                                        start=(g == 0), stop=(g == 1))
                f0 = first_feature(n) + ft * P
                drain(bk, dw_out[gate][f0:f0 + P, :])

        def transpose_dz(q, s, kind):
            words = tiles["dz", q, s][:].rearrange("p j f -> p (j f)").bitcast(F32)
            per_j = K_PASS // 2
            for jp in range(2):
                bk = bank(kind, [P, 2, 2, P], F32)
                for jj in range(2):
                    w0 = (2 * jp + jj) * per_j
                    for u in range(2):
                        nc.tensor.transpose(bk[:, jj, u, :], words[:, w0 + u:w0 + per_j:2], ident[:])
                tiles["dz_turned", q, s, jp] = bk

        def group_features(q, s):
            grouped = ring("feature_grouped", 3, [P, K_PASS * PACK], BF16)
            grouped_words = grouped[:].bitcast(F32).rearrange("q (j p u) -> q j p u", j=PACK, u=2)
            for jp in range(2):
                nc.scalar.copy(out=grouped_words[:, 2 * jp:2 * jp + 2, :, :],
                               in_=tiles["dz_turned", q, s, jp][:].rearrange("q j u p -> q j p u"))
            tiles["feature_grouped", q, s] = grouped

        def turn_dz(q, s):
            transpose_dz(q, s, "tr")
            group_features(q, s)

        def quantise_features(q, s):
            codes = ring("feature_codes", 9, [P, K_PASS], U32)
            scales = ring("feature_scales", 9, [P, K_PASS], U8)
            nc.vector.quantize_mx(out=codes[:].bitcast(E5M2), scales=scales[:], in_=tiles["feature_grouped", q, s][:])
            tiles["feature_q", q, s] = (codes, scales)

        def dx_passes(g, j, passes, open_in, closes):
            if open_in:
                tiles["dx", g, j] = bank(open_in, [P, I], F32)
            cols = slice(j * P, (j + 1) * P)
            for k in passes:
                half, s = divmod(k, 3)
                codes, scales = tiles["feature_q", 2 * half + g, s]
                nc.tensor.matmul_mx(out=tiles["dx", g, j][:], lhsT=codes[:, cols].bitcast(E5M2), lhsT_scale=scales[:, cols],
                                    rhs=op_codes[:, 2 + k, :].bitcast(E4M3), rhs_scale=op_scales[:, 2 + k, :],
                                    start=(bool(open_in) and k == passes[0]), stop=(closes and k == passes[-1]))

        dx_parked = sb.tile([P, PACK, I], F32, name="dx_parked", align_bytes=64)

        def dx_park(j):
            dx_passes(1, j, (0, 1, 2), "mx", True)
            nc.scalar.copy(out=dx_parked[:, j, :], in_=tiles["dx", 1, j][:])

        def dx_finish(j):
            nc.vector.tensor_tensor(out=dx_parked[:, j, :], in0=tiles["dx", 1, j][:], in1=dx_parked[:, j, :], op=ALU.add)
            nc.sync.dma_start(out=dx_rows[1, :, j, :], in_=dx_parked[:, j, :])

        load_ig(0, 0, P)
        load_f(0, 0, P)
        load_c0(0)
        load_ig(0, P, CW)
        load_f(0, P, CW)
        load_grad(0)
        nc.vector.memset(last_rows[:].rearrange("p k w -> p (k w)").bitcast(U32), 0)
        make_identity(nc, ident[:])
        make_identity(nc, ident_bf[:])
        load_last_step(0)
        load_operand(0)
        load_f(1)
        load_ig(1)
        load_c0(1)
        load_f(2)
        load_grad(1)
        load_operand(1)

        for ft in range(FT):
            product_b(0, ft * P, (ft + 1) * P)
            product_a(0, nc.vector, ft * P, (ft + 1) * P)
            cell_state(0, (ft,))
            if ft == 0:
                square_g(0)
            tanh_c(0, (ft,))
            square_h(0, ft, ft + 1)
        turn_last_step(0)
        factor_g(0)
        factor_i(0)
        load_ig(2)
        group_operand(0, "scalar", 0, I)

        for n in range(LAST):
            turns = passes_completed_by(n - 1)
            turns_first = turns if n == DX0_PERIOD else []
            turns_later = [] if n == DX0_PERIOD else turns
            dc_feature_major(n)
            if n > 0:
                load_ig(n + 2)
            if n % 2 == 0 and n // 2 + 1 < QUARTERS:
                load_last_step(n // 2 + 1)
            load_grad(n + 2)
            load_f(n + 3)
            if n % 2 == 1:
                load_c0(n // 2 + 2)
            for k in operands_at(n, 2, PARK_PERIOD - 1):
                load_operand(k)
            for q, s in turns_first[:1]:
                turn_dz(q, s)
            if n > 0:
                group_tokens(n - 1, first, "scalar")
            dc_token_major(n)
            if n == 0:
                product_a(1, nc.vector)
                factor_f(0)
            product_b(n + 1)
            for q, s in turns_first[1:]:
                turn_dz(q, s)
            if n > 0:
                group_tokens(n - 1, second, "scalar")
            cell_state(n + 1)
            if n > 0:
                group_tokens(n - 1, third, "scalar")
            for q, s in passes_completed_by(n - 2):
                quantise_features(q, s)
            if n > 0:
                factor_i(n)
            if n == 1:
                quantise_operand(0)
            if n > 0:
                for k in operands_at(n, 0, DX0_PERIOD):
                    quantise_operand(k)
            if n == 0:
                for ft in range(FT):
                    tanh_c(1, (ft,))
                    square_h(1, ft, ft + 1)
            else:
                tanh_c(n + 1)
            if n > 0 and token_pass(n - 1) == 1:
                quantise_all_gates(n - 1)
            if n == DX0_PERIOD:
                factor_g(n)
                quantise_features(*turns_first[0])
                factor_f(n)
                quantise_features(*turns_first[1])
                for j in (0, 1):
                    dx_passes(0, j, (3, 4, 5), None, True)
                for j in (2, 3):
                    dx_passes(0, j, range(6), "ct", True)
            elif n > 0:
                factor_f(n)
                factor_g(n)
            product_a(n + 2, nc.gpsimd)
            for k, pool_end, vector_end in operand_shares(n):
                group_operand(k, "gpsimd", 0, pool_end)
            for gate in GATE_ORDER:
                round_dz(n, gate)
            if n > 0 and token_pass(n - 1) == 0:
                quantise_all_gates(n - 1)
            for place, gate in enumerate(GATE_ORDER):
                for q, s in turns_later[place:place + 1]:
                    turn_dz(q, s)
                if place == 0 and n > 0:
                    square_h(n + 1)
                    if n % 2 == 1:
                        turn_last_step(n // 2 + 1)
                if place == 1:
                    square_g(n + 1)
                if n in DW_PERIODS:
                    weight_gradient(n - 1, gate, "mx")
                if n == PARK_PERIOD:
                    for j in range(PACK)[2 * place:2 * place + 2]:
                        dx_park(j)
            for k, pool_end, vector_end in operand_shares(n):
                group_operand(k, "vector", pool_end, vector_end)
                group_operand(k, "scalar", vector_end, I)
            if n == PARK_PERIOD:
                for j in (0, 1):
                    dx_passes(0, j, (0, 1, 2), "mx", False)
            if n == DX0_PERIOD:
                for j in range(PACK):
                    drain(tiles["dx", 0, j], dx_rows[0, :, j, :])

        q = QUARTERS - 1
        dc_feature_major(LAST)
        for gate in GATE_ORDER:
            group_tokens(LAST - 1, gate, "scalar")
        dc_token_major(LAST)
        turn_dz(q, 0)
        factor_i(LAST)
        factor_g(LAST)
        quantise_all_gates(LAST - 1)
        factor_f(LAST)
        quantise_features(q, 0)
        for gate, kind in ((first, "mx"), (second, "ct"), (third, "mx")):
            weight_gradient(LAST - 1, gate, kind)
        round_dz(LAST, first)
        transpose_dz(q, 1, "tr")
        for j in (0, 1):
            dx_passes(1, j, (3,), "ct", False)
        round_dz(LAST, second)
        round_dz(LAST, third)
        transpose_dz(q, 2, "dc")
        for j in (2, 3):
            dx_passes(1, j, (3,), "mx", False)
        group_features(q, 1)
        group_features(q, 2)
        group_tokens(LAST, first, "vector")
        group_tokens(LAST, second, "vector")
        quantise_tokens(LAST, 0, 1)
        group_tokens(LAST, third, "vector")
        quantise_tokens(LAST, 1, 2)
        quantise_features(q, 1)
        quantise_features(q, 2)
        quantise_tokens(LAST, 2, 3)
        weight_gradient(LAST, first, "tr")
        weight_gradient(LAST, second, "dc")
        for j in range(PACK):
            dx_passes(1, j, (4, 5), None, True)
            dx_finish(j)
        weight_gradient(LAST, third, "tr")
